import numpy as np
import ml_dtypes


def mxq(x, axis, fmt="e4m3"):
    dtype, down = {"e4m3": (ml_dtypes.float8_e4m3fn, 7), "e5m2": (ml_dtypes.float8_e5m2, 14)}[fmt]
    v = np.moveaxis(np.asarray(x, np.float32).astype(ml_dtypes.bfloat16).astype(np.float64), axis, -1)
    blocks = v.reshape(v.shape[:-1] + (-1, 32))
    amax = np.abs(blocks).max(-1, keepdims=True)
    byte = np.maximum(np.where(amax > 0, np.frexp(amax)[1] - 1 + 127, 0) - down, 1)
    scale = np.exp2(byte - 127.0)
    codes = (blocks / scale).astype(np.float32).astype(dtype).astype(np.float64)
    return np.moveaxis((codes * scale).reshape(v.shape), -1, axis)


WIDE = False


def mx_kscale(k):
    if not WIDE:
        return np.ones(k)
    levels = np.array([10, -10, 5, -5, 0])
    a = np.random.permutation(np.resize(levels, k // 512 * 4)).reshape(k // 512, 4)
    idx = np.arange(k)
    return np.exp2(a[idx // 512, idx % 128 // 32])


BF16 = ml_dtypes.bfloat16


def bf(x):
    return np.asarray(x, np.float32).astype(BF16)


def f64(x):
    return np.asarray(x).astype(np.float64)


E2M1 = np.array([0.0, 0.5, 1.0, 1.5, 2.0, 3.0, 4.0, 6.0, -0.0, -0.5, -1.0, -1.5, -2.0, -3.0, -4.0, -6.0])


def pack_weight(w, fmt):
    k, n = w.shape
    w = f64(bf(w)).reshape(k // 32, 32, n)
    amax = np.abs(w).max(1)
    if fmt == "e4m3":
        byte = np.frexp(amax)[1] - 1 + 127 - 7
    else:
        mant, ex = np.frexp(amax / 6.0)
        byte = np.where(mant > 0.5, ex, ex - 1) + 127
    byte = np.clip(np.where(amax > 0, byte, 1), 1, 254)
    scaled = (w * np.exp2(127.0 - byte)[:, None, :]).reshape(k, n).astype(np.float32)
    by_word = np.ascontiguousarray(scaled.reshape(k // 512, 128, 4, n).transpose(0, 1, 3, 2))
    if fmt == "e4m3":
        words = by_word.astype(ml_dtypes.float8_e4m3fn).view(np.uint8)
    else:
        c = by_word.astype(ml_dtypes.float4_e2m1fn).view(np.uint8) & 0xF
        words = c[..., 0::2] | (c[..., 1::2] << 4)
    return np.ascontiguousarray(words), np.ascontiguousarray(byte.astype(np.uint8).reshape(k // 512, 16, n))


def unpack_weight(words, scales, fmt):
    g, p, n, _ = words.shape
    if fmt == "e4m3":
        vals = np.ascontiguousarray(words).view(ml_dtypes.float8_e4m3fn).astype(np.float64)
    else:
        nib = np.empty((g, p, n, 4), np.uint8)
        nib[..., 0::2] = words & 0xF
        nib[..., 1::2] = words >> 4
        vals = E2M1[nib]
    vals = vals * np.repeat(np.exp2(scales.astype(np.float64) - 127.0), 8, axis=1)[..., None]
    return vals.transpose(0, 1, 3, 2).reshape(g * 512, n)

def pack4(w):
    words, scales = pack_weight(w, "e2m1")
    return words.reshape(words.shape[0], 128, -1), scales


def unpack4(words, scales):
    return unpack_weight(words.reshape(words.shape[0], 128, -1, 2), scales, "e2m1")


B, S, C, HD = 4, 1024, 1024, 128
H = C // HD
HP = HD // 2
EPS = 1e-6
THETA = 10000.0


def rmsnorm(h, g):
    return h * (1.0 / np.sqrt(np.mean(h * h, axis=-1, keepdims=True) + EPS)) * g


def apply_rope1(h, freqs):
    sh = h.shape
    h_ = h.reshape(*sh[:-1], -1, 1, 2)
    out = freqs[..., 0] * h_[..., 0] + freqs[..., 1] * h_[..., 1]
    return out.reshape(sh)


def setup_inputs():
    s = mx_kscale(C)
    pos = f64(np.random.randint(0, S, size=(S, 1)))
    inv_freq = 1.0 / THETA ** (np.arange(HP) / HP)
    ang = pos * inv_freq
    cos, sin = np.cos(ang), np.sin(ang)
    rot = np.stack([np.stack([cos, -sin], -1), np.stack([sin, cos], -1)], -2)
    x = bf(np.random.standard_normal((B, S, C)) * s)
    w = np.random.standard_normal((C, C)) / np.sqrt(C) / s[None, :]
    w_words, w_scales = pack4(np.ascontiguousarray(w.T))
    return {"x": x,
            "freqs": bf(rot[None, :, None]),
            "w_words": w_words,
            "w_scales": w_scales,
            "b": bf(np.random.standard_normal(C) * 0.3),
            "g": bf(1.0 + 0.1 * np.random.standard_normal(HD))}


def reference(x, freqs, w_words, w_scales, b, g):
    p = (mxq(f64(x), 2, "e4m3") @ unpack4(w_words, w_scales)) + f64(b)
    h = p.reshape(B, S, H, HD)
    return apply_rope1(rmsnorm(h, f64(g)), f64(freqs))

@@ -1,0 +1,163 @@
+from contextlib import ExitStack
+
+import concourse.mybir as mybir
+from concourse.masks import make_identity
+
+F32 = mybir.dt.float32
+BF16 = mybir.dt.bfloat16
+I32 = mybir.dt.int32
+U32 = mybir.dt.uint32
+U8 = mybir.dt.uint8
+FP8X4 = mybir.dt.float8_e4m3fn_x4
+FP4X4 = mybir.dt.float4_e2m1fn_x4
+ACT = mybir.ActivationFunctionType
+ALU = mybir.AluOpType
+
+P = 128
+BATCH, SEQ, CH = 4, 1024, 1024
+HEADS, HEAD_DIM = 8, 128
+PAIRS = HEAD_DIM // 2
+EPS = 1e-6
+K_PASS = 512
+PASSES = CH // K_PASS
+N_BANK = 512
+BANKS = CH // N_BANK
+SEQ_TILES = SEQ // P
+
+FLOPS = 2 * BATCH * SEQ * CH * CH
+
+
+def tile_selfattention_pa_t_kernel(tc, x, freqs, w_words, w_scales, b, g, out):
+    nc = tc.nc
+    with ExitStack() as ctx:
+        const = ctx.enter_context(tc.tile_pool(name="const", bufs=1))
+        x_pool = ctx.enter_context(tc.tile_pool(name="x_pool", bufs=SEQ_TILES))
+        quant = ctx.enter_context(tc.tile_pool(name="quant", bufs=3))
+        work = ctx.enter_context(tc.tile_pool(name="work", bufs=3))
+        small = ctx.enter_context(tc.tile_pool(name="small", bufs=4))
+        psum_x = ctx.enter_context(tc.psum_pool(name="psum_x", bufs=2))
+        psum_acc = ctx.enter_context(tc.psum_pool(name="psum_acc", bufs=4))
+        psum_tab = ctx.enter_context(tc.psum_pool(name="psum_tab", bufs=2))
+
+        w_planes = const.tile([P, PASSES, CH], U8, align_bytes=64)
+        nc.vector.memset(w_planes[:].rearrange("p g n -> p (g n)").bitcast(I32), 0)
+        scale_rows = w_scales.bitcast(I32)
+        for quadrant in range(4):
+            nc.sync.dma_start(
+                out=w_planes[32 * quadrant : 32 * quadrant + 4, :, :].bitcast(I32),
+                in_=scale_rows[:, 4 * quadrant : 4 * quadrant + 4, :].rearrange("g r n -> r g n"),
+            )
+        w_sb = const.tile([P, PASSES, 2 * CH], U8, align_bytes=64)
+        nc.sync.dma_start(out=w_sb[:].bitcast(I32), in_=w_words.bitcast(I32).rearrange("g p n -> p g n"))
+
+        x_blocks = x.rearrange("n (s p) k -> s p n k", p=P)
+        x_sb = []
+        for s in range(SEQ_TILES):
+            x_tile = x_pool.tile([P, BATCH, CH], BF16, name="x_tile")
+            nc.sync.dma_start(out=x_tile[:], in_=x_blocks[s])
+            x_sb.append(x_tile)
+
+        freqs_sb = const.tile([P, SEQ_TILES, 4 * PAIRS], BF16)
+        nc.scalar.dma_start(out=freqs_sb[:], in_=freqs[0, :, 0].rearrange("(s p) j i k -> p s (j i k)", p=P))
+
+        bias_bc = const.tile([P, CH], BF16)
+        nc.scalar.dma_start(out=bias_bc[:], in_=b.partition_broadcast(P))
+        gain_bc = const.tile([P, HEAD_DIM], BF16)
+        nc.scalar.dma_start(out=gain_bc[:], in_=g.partition_broadcast(P))
+
+        ident = const.tile([P, P], F32)
+        make_identity(nc, ident[:])
+        eps_col = const.tile([P, 1], F32)
+        nc.vector.memset(eps_col[:], EPS)
+
+        table = const.tile([P, SEQ_TILES, 2 * HEAD_DIM], F32)
+        for s in range(SEQ_TILES):
+            nc.gpsimd.tensor_tensor(
+                out=table[:, s, :].rearrange("p (k j i) -> p k j i", k=2, j=PAIRS, i=2),
+                in0=freqs_sb[:, s, :].rearrange("p (j i k) -> p k j i", j=PAIRS, i=2, k=2),
+                in1=gain_bc[:]
+                .rearrange("p (j k o) -> p k j o", j=PAIRS, k=2, o=1)
+                .to_broadcast([P, 2, PAIRS, 2]),
+                op=ALU.mult,
+            )
+
+        for s in range(SEQ_TILES):
+            tab = psum_tab.tile([P, 2 * HEAD_DIM], F32)
+            nc.tensor.matmul(out=tab[:], lhsT=ident[:], rhs=table[:, s, :], start=True, stop=True)
+
+            for n in range(BATCH):
+                x_words = x_sb[s][:, n, :].bitcast(F32)
+                xt = psum_x.tile([P, PASSES, 2, P], F32)
+                for gp in range(PASSES):
+                    for u in range(2):
+                        nc.tensor.transpose(
+                            xt[:, gp, u, :],
+                            x_words[:, 256 * gp + u : 256 * (gp + 1) : 2],
+                            ident[:],
+                        )
+                grouped = quant.tile([P, PASSES * P * 4], BF16, align_bytes=64)
+                nc.scalar.copy(
+                    out=grouped[:].bitcast(F32).rearrange("p (g r u) -> p g r u", g=PASSES, r=P, u=2),
+                    in_=xt[:].rearrange("p g u r -> p g r u"),
+                )
+                x_codes = quant.tile([P, PASSES * P], U32, align_bytes=64)
+                x_scales = quant.tile([P, PASSES * P], U8, align_bytes=64)
+                nc.vector.quantize_mx(out=x_codes[:].bitcast(FP8X4), scales=x_scales[:], in_=grouped[:])
+
+                u_sb = work.tile([P, CH], F32)
+                for bank in range(BANKS):
+                    acc = psum_acc.tile([P, N_BANK], F32)
+                    for gp in range(PASSES):
+                        nc.tensor.matmul_mx(
+                            out=acc[:],
+                            lhsT=x_codes[:, P * gp : P * (gp + 1)].bitcast(FP8X4),
+                            lhsT_scale=x_scales[:, P * gp : P * (gp + 1)],
+                            rhs=w_sb[:, gp, 2 * N_BANK * bank : 2 * N_BANK * (bank + 1)].bitcast(FP4X4),
+                            rhs_scale=w_planes[:, gp, N_BANK * bank : N_BANK * (bank + 1)],
+                            start=(gp == 0),
+                            stop=(gp == PASSES - 1),
+                        )
+                    cols = slice(N_BANK * bank, N_BANK * (bank + 1))
+                    nc.vector.tensor_tensor(out=u_sb[:, cols], in0=acc[:], in1=bias_bc[:, cols], op=ALU.add)
+
+                sum_sq = small.tile([P, HEADS], F32)
+                for h in range(HEADS):
+                    squares = small.tile([P, HEAD_DIM], BF16)
+                    nc.scalar.activation(
+                        out=squares[:],
+                        in_=u_sb[:, HEAD_DIM * h : HEAD_DIM * (h + 1)],
+                        func=ACT.Square,
+                        accum_out=sum_sq[:, h : h + 1],
+                    )
+                rms = small.tile([P, HEADS], F32)
+                nc.scalar.activation(
+                    out=rms[:], in_=sum_sq[:], func=ACT.Sqrt, bias=eps_col[:, 0:1], scale=1.0 / HEAD_DIM
+                )
+                rstd = small.tile([P, HEADS], F32)
+                nc.vector.reciprocal(out=rstd[:], in_=rms[:])
+
+                u_pairs = u_sb[:].rearrange("p (h j k) -> p h j k", h=HEADS, j=PAIRS, k=2)
+                full = [P, HEADS, PAIRS, 2]
+                terms = []
+                for k in range(2):
+                    term = work.tile([P, CH], F32, name="term%d" % k)
+                    nc.vector.tensor_tensor(
+                        out=term[:].rearrange("p (h j i) -> p h j i", h=HEADS, j=PAIRS, i=2),
+                        in0=u_pairs[:, :, :, k : k + 1].to_broadcast(full),
+                        in1=tab[:, HEAD_DIM * k : HEAD_DIM * (k + 1)]
+                        .rearrange("p (o j i) -> p o j i", o=1, j=PAIRS, i=2)
+                        .to_broadcast(full),
+                        op=ALU.mult,
+                    )
+                    terms.append(term)
+                nc.gpsimd.tensor_tensor(out=terms[0][:], in0=terms[0][:], in1=terms[1][:], op=ALU.add)
+
+                result = work.tile([P, CH], F32)
+                for h in range(HEADS):
+                    cols = slice(HEAD_DIM * h, HEAD_DIM * (h + 1))
+                    nc.scalar.activation(
+                        out=result[:, cols], in_=terms[0][:, cols], func=ACT.Copy, scale=rstd[:, h : h + 1]
+                    )
+                nc.sync.dma_start(
+                    out=out[n, P * s : P * (s + 1)].rearrange("p h c -> p (h c)"), in_=result[:]
+                )

@@ -23,6 +23,8 @@ PASSES = CH // K_PASS
 N_BANK = 512
 BANKS = CH // N_BANK
 SEQ_TILES = SEQ // P
+TILES = SEQ_TILES * BATCH
+SCALAR_HEADS = 2
 
 FLOPS = 2 * BATCH * SEQ * CH * CH
 
@@ -30,15 +32,23 @@ FLOPS = 2 * BATCH * SEQ * CH * CH
 def tile_selfattention_pa_t_kernel(tc, x, freqs, w_words, w_scales, b, g, out):
     nc = tc.nc
     with ExitStack() as ctx:
+        ctx.enter_context(tc.manual_schedule())
         const = ctx.enter_context(tc.tile_pool(name="const", bufs=1))
-        x_pool = ctx.enter_context(tc.tile_pool(name="x_pool", bufs=SEQ_TILES))
+        x_pool = ctx.enter_context(tc.tile_pool(name="x_pool", bufs=TILES))
         quant = ctx.enter_context(tc.tile_pool(name="quant", bufs=3))
         work = ctx.enter_context(tc.tile_pool(name="work", bufs=3))
         small = ctx.enter_context(tc.tile_pool(name="small", bufs=4))
         psum_x = ctx.enter_context(tc.psum_pool(name="psum_x", bufs=2))
-        psum_acc = ctx.enter_context(tc.psum_pool(name="psum_acc", bufs=4))
+        psum_acc = ctx.enter_context(tc.psum_pool(name="psum_acc", bufs=2 * BANKS))
         psum_tab = ctx.enter_context(tc.psum_pool(name="psum_tab", bufs=2))
 
+        def load_x(i):
+            x_tile = x_pool.tile([P, CH], BF16, name="x_tile")
+            s, n = divmod(i, BATCH)
+            nc.sync.dma_start(out=x_tile[:], in_=x[n, P * s : P * (s + 1), :])
+            return x_tile
+
+        x_sb = [load_x(0)]
         w_planes = const.tile([P, PASSES, CH], U8, align_bytes=64)
         nc.vector.memset(w_planes[:].rearrange("p g n -> p (g n)").bitcast(I32), 0)
         scale_rows = w_scales.bitcast(I32)
@@ -49,21 +59,15 @@ def tile_selfattention_pa_t_kernel(tc, x, freqs, w_words, w_scales, b, g, out):
             )
         w_sb = const.tile([P, PASSES, 2 * CH], U8, align_bytes=64)
         nc.sync.dma_start(out=w_sb[:].bitcast(I32), in_=w_words.bitcast(I32).rearrange("g p n -> p g n"))
-
-        x_blocks = x.rearrange("n (s p) k -> s p n k", p=P)
-        x_sb = []
-        for s in range(SEQ_TILES):
-            x_tile = x_pool.tile([P, BATCH, CH], BF16, name="x_tile")
-            nc.sync.dma_start(out=x_tile[:], in_=x_blocks[s])
-            x_sb.append(x_tile)
+        for i in range(1, TILES):
+            x_sb.append(load_x(i))
 
         freqs_sb = const.tile([P, SEQ_TILES, 4 * PAIRS], BF16)
         nc.scalar.dma_start(out=freqs_sb[:], in_=freqs[0, :, 0].rearrange("(s p) j i k -> p s (j i k)", p=P))
-
-        bias_bc = const.tile([P, CH], BF16)
-        nc.scalar.dma_start(out=bias_bc[:], in_=b.partition_broadcast(P))
         gain_bc = const.tile([P, HEAD_DIM], BF16)
         nc.scalar.dma_start(out=gain_bc[:], in_=g.partition_broadcast(P))
+        bias_bc = const.tile([P, CH], BF16)
+        nc.scalar.dma_start(out=bias_bc[:], in_=b.partition_broadcast(P))
 
         ident = const.tile([P, P], F32)
         make_identity(nc, ident[:])
@@ -81,83 +85,129 @@ def tile_selfattention_pa_t_kernel(tc, x, freqs, w_words, w_scales, b, g, out):
                 op=ALU.mult,
             )
 
-        for s in range(SEQ_TILES):
-            tab = psum_tab.tile([P, 2 * HEAD_DIM], F32)
-            nc.tensor.matmul(out=tab[:], lhsT=ident[:], rhs=table[:, s, :], start=True, stop=True)
+        xt, grouped, x_codes, x_scales, acc, u_sb, rms, rstd, terms, tab = {}, {}, {}, {}, {}, {}, {}, {}, {}, {}
 
-            for n in range(BATCH):
-                x_words = x_sb[s][:, n, :].bitcast(F32)
-                xt = psum_x.tile([P, PASSES, 2, P], F32)
+        def transposes(i):
+            x_words = x_sb[i][:].bitcast(F32)
+            xt[i] = psum_x.tile([P, PASSES, 2, P], F32, name="xt")
+            for gp in range(PASSES):
+                for u in range(2):
+                    nc.tensor.transpose(
+                        xt[i][:, gp, u, :], x_words[:, 256 * gp + u : 256 * (gp + 1) : 2], ident[:]
+                    )
+
+        def regroup(i):
+            grouped[i] = quant.tile([P, PASSES * P * 4], BF16, align_bytes=64, name="grouped")
+            nc.scalar.copy(
+                out=grouped[i][:].bitcast(F32).rearrange("p (g r u) -> p g r u", g=PASSES, r=P, u=2),
+                in_=xt[i][:].rearrange("p g u r -> p g r u"),
+            )
+
+        def quantise(i):
+            x_codes[i] = quant.tile([P, PASSES * P], U32, align_bytes=64, name="x_codes")
+            x_scales[i] = quant.tile([P, PASSES * P], U8, align_bytes=64, name="x_scales")
+            nc.vector.quantize_mx(
+                out=x_codes[i][:].bitcast(FP8X4), scales=x_scales[i][:], in_=grouped[i][:]
+            )
+
+        def multiply(i):
+            acc[i] = []
+            for bank in range(BANKS):
+                acc_bank = psum_acc.tile([P, N_BANK], F32, name="acc_bank")
                 for gp in range(PASSES):
-                    for u in range(2):
-                        nc.tensor.transpose(
-                            xt[:, gp, u, :],
-                            x_words[:, 256 * gp + u : 256 * (gp + 1) : 2],
-                            ident[:],
-                        )
-                grouped = quant.tile([P, PASSES * P * 4], BF16, align_bytes=64)
-                nc.scalar.copy(
-                    out=grouped[:].bitcast(F32).rearrange("p (g r u) -> p g r u", g=PASSES, r=P, u=2),
-                    in_=xt[:].rearrange("p g u r -> p g r u"),
-                )
-                x_codes = quant.tile([P, PASSES * P], U32, align_bytes=64)
-                x_scales = quant.tile([P, PASSES * P], U8, align_bytes=64)
-                nc.vector.quantize_mx(out=x_codes[:].bitcast(FP8X4), scales=x_scales[:], in_=grouped[:])
-
-                u_sb = work.tile([P, CH], F32)
-                for bank in range(BANKS):
-                    acc = psum_acc.tile([P, N_BANK], F32)
-                    for gp in range(PASSES):
-                        nc.tensor.matmul_mx(
-                            out=acc[:],
-                            lhsT=x_codes[:, P * gp : P * (gp + 1)].bitcast(FP8X4),
-                            lhsT_scale=x_scales[:, P * gp : P * (gp + 1)],
-                            rhs=w_sb[:, gp, 2 * N_BANK * bank : 2 * N_BANK * (bank + 1)].bitcast(FP4X4),
-                            rhs_scale=w_planes[:, gp, N_BANK * bank : N_BANK * (bank + 1)],
-                            start=(gp == 0),
-                            stop=(gp == PASSES - 1),
-                        )
-                    cols = slice(N_BANK * bank, N_BANK * (bank + 1))
-                    nc.vector.tensor_tensor(out=u_sb[:, cols], in0=acc[:], in1=bias_bc[:, cols], op=ALU.add)
-
-                sum_sq = small.tile([P, HEADS], F32)
-                for h in range(HEADS):
-                    squares = small.tile([P, HEAD_DIM], BF16)
-                    nc.scalar.activation(
-                        out=squares[:],
-                        in_=u_sb[:, HEAD_DIM * h : HEAD_DIM * (h + 1)],
-                        func=ACT.Square,
-                        accum_out=sum_sq[:, h : h + 1],
+                    nc.tensor.matmul_mx(
+                        out=acc_bank[:],
+                        lhsT=x_codes[i][:, P * gp : P * (gp + 1)].bitcast(FP8X4),
+                        lhsT_scale=x_scales[i][:, P * gp : P * (gp + 1)],
+                        rhs=w_sb[:, gp, 2 * N_BANK * bank : 2 * N_BANK * (bank + 1)].bitcast(FP4X4),
+                        rhs_scale=w_planes[:, gp, N_BANK * bank : N_BANK * (bank + 1)],
+                        start=(gp == 0),
+                        stop=(gp == PASSES - 1),
                     )
-                rms = small.tile([P, HEADS], F32)
+                acc[i].append(acc_bank)
+
+        def table_to_psum(s):
+            tab[s] = psum_tab.tile([P, 2 * HEAD_DIM], F32, name="tab")
+            nc.tensor.matmul(out=tab[s][:], lhsT=ident[:], rhs=table[:, s, :], start=True, stop=True)
+
+        def add_bias(i):
+            u_sb[i] = work.tile([P, CH], F32, name="u_sb")
+            for bank in range(BANKS):
+                cols = slice(N_BANK * bank, N_BANK * (bank + 1))
+                nc.vector.tensor_tensor(
+                    out=u_sb[i][:, cols], in0=acc[i][bank][:], in1=bias_bc[:, cols], op=ALU.add
+                )
+
+        def statistics(i):
+            sum_sq = small.tile([P, HEADS], F32, name="sum_sq")
+            for h in range(HEADS):
+                squares = small.tile([P, HEAD_DIM], BF16, name="squares")
                 nc.scalar.activation(
-                    out=rms[:], in_=sum_sq[:], func=ACT.Sqrt, bias=eps_col[:, 0:1], scale=1.0 / HEAD_DIM
+                    out=squares[:],
+                    in_=u_sb[i][:, HEAD_DIM * h : HEAD_DIM * (h + 1)],
+                    func=ACT.Square,
+                    accum_out=sum_sq[:, h : h + 1],
                 )
-                rstd = small.tile([P, HEADS], F32)
-                nc.vector.reciprocal(out=rstd[:], in_=rms[:])
+            rms[i] = small.tile([P, HEADS], F32, name="rms")
+            nc.scalar.activation(
+                out=rms[i][:], in_=sum_sq[:], func=ACT.Sqrt, bias=eps_col[:, 0:1], scale=1.0 / HEAD_DIM
+            )
 
-                u_pairs = u_sb[:].rearrange("p (h j k) -> p h j k", h=HEADS, j=PAIRS, k=2)
-                full = [P, HEADS, PAIRS, 2]
-                terms = []
-                for k in range(2):
-                    term = work.tile([P, CH], F32, name="term%d" % k)
-                    nc.vector.tensor_tensor(
-                        out=term[:].rearrange("p (h j i) -> p h j i", h=HEADS, j=PAIRS, i=2),
-                        in0=u_pairs[:, :, :, k : k + 1].to_broadcast(full),
-                        in1=tab[:, HEAD_DIM * k : HEAD_DIM * (k + 1)]
-                        .rearrange("p (o j i) -> p o j i", o=1, j=PAIRS, i=2)
-                        .to_broadcast(full),
-                        op=ALU.mult,
-                    )
-                    terms.append(term)
-                nc.gpsimd.tensor_tensor(out=terms[0][:], in0=terms[0][:], in1=terms[1][:], op=ALU.add)
+        def reciprocal(i):
+            rstd[i] = small.tile([P, HEADS], F32, name="rstd")
+            nc.vector.reciprocal(out=rstd[i][:], in_=rms[i][:])
 
-                result = work.tile([P, CH], F32)
-                for h in range(HEADS):
-                    cols = slice(HEAD_DIM * h, HEAD_DIM * (h + 1))
-                    nc.scalar.activation(
-                        out=result[:, cols], in_=terms[0][:, cols], func=ACT.Copy, scale=rstd[:, h : h + 1]
-                    )
-                nc.sync.dma_start(
-                    out=out[n, P * s : P * (s + 1)].rearrange("p h c -> p (h c)"), in_=result[:]
+        def rotate(i):
+            u_pairs = u_sb[i][:].rearrange("p (h j k) -> p h j k", h=HEADS, j=PAIRS, k=2)
+            full = [P, HEADS, PAIRS, 2]
+            terms[i] = []
+            for k in range(2):
+                term = work.tile([P, CH], F32, name="term%d" % k)
+                nc.vector.tensor_tensor(
+                    out=term[:].rearrange("p (h j i) -> p h j i", h=HEADS, j=PAIRS, i=2),
+                    in0=u_pairs[:, :, :, k : k + 1].to_broadcast(full),
+                    in1=tab[i // BATCH][:, HEAD_DIM * k : HEAD_DIM * (k + 1)]
+                    .rearrange("p (o j i) -> p o j i", o=1, j=PAIRS, i=2)
+                    .to_broadcast(full),
+                    op=ALU.mult,
                 )
+                terms[i].append(term)
+
+        def add_terms(i):
+            nc.gpsimd.tensor_tensor(out=terms[i][0][:], in0=terms[i][0][:], in1=terms[i][1][:], op=ALU.add)
+
+        def scale_and_store(i):
+            rotated = terms[i][0]
+            result = work.tile([P, CH], F32, name="result")
+            for h in range(SCALAR_HEADS):
+                cols = slice(HEAD_DIM * h, HEAD_DIM * (h + 1))
+                nc.scalar.activation(
+                    out=result[:, cols], in_=rotated[:, cols], func=ACT.Copy, scale=rstd[i][:, h : h + 1]
+                )
+            rest = slice(HEAD_DIM * SCALAR_HEADS, CH)
+            nc.gpsimd.tensor_tensor(
+                out=result[:, rest].rearrange("p (h c) -> p h c", c=HEAD_DIM),
+                in0=rotated[:, rest].rearrange("p (h c) -> p h c", c=HEAD_DIM),
+                in1=rstd[i][:, SCALAR_HEADS:HEADS].unsqueeze(2).to_broadcast([P, HEADS - SCALAR_HEADS, HEAD_DIM]),
+                op=ALU.mult,
+            )
+            s, n = divmod(i, BATCH)
+            nc.sync.dma_start(out=out[n, P * s : P * (s + 1)].rearrange("p h c -> p (h c)"), in_=result[:])
+
+        def run(stage, i):
+            if 0 <= i < TILES:
+                stage(i)
+
+        for step in range(-3, TILES + 1):
+            run(multiply, step + 1)
+            if (step + 1) % BATCH == 0 and step + 1 < TILES:
+                table_to_psum((step + 1) // BATCH)
+            run(transposes, step + 3)
+            run(regroup, step + 2)
+            run(rotate, step)
+            run(quantise, step + 2)
+            run(add_bias, step + 1)
+            run(statistics, step)
+            run(reciprocal, step)
+            run(add_terms, step - 1)
+            run(scale_and_store, step - 1)

@@ -24,8 +24,6 @@ N_BANK = 512
 BANKS = CH // N_BANK
 SEQ_TILES = SEQ // P
 TILES = SEQ_TILES * BATCH
-SCALAR_HEADS = 2
-
 FLOPS = 2 * BATCH * SEQ * CH * CH
 
 
@@ -179,18 +177,11 @@ def tile_selfattention_pa_t_kernel(tc, x, freqs, w_words, w_scales, b, g, out):
         def scale_and_store(i):
             rotated = terms[i][0]
             result = work.tile([P, CH], F32, name="result")
-            for h in range(SCALAR_HEADS):
+            for h in range(HEADS):
                 cols = slice(HEAD_DIM * h, HEAD_DIM * (h + 1))
                 nc.scalar.activation(
                     out=result[:, cols], in_=rotated[:, cols], func=ACT.Copy, scale=rstd[i][:, h : h + 1]
                 )
-            rest = slice(HEAD_DIM * SCALAR_HEADS, CH)
-            nc.gpsimd.tensor_tensor(
-                out=result[:, rest].rearrange("p (h c) -> p h c", c=HEAD_DIM),
-                in0=rotated[:, rest].rearrange("p (h c) -> p h c", c=HEAD_DIM),
-                in1=rstd[i][:, SCALAR_HEADS:HEADS].unsqueeze(2).to_broadcast([P, HEADS - SCALAR_HEADS, HEAD_DIM]),
-                op=ALU.mult,
-            )
             s, n = divmod(i, BATCH)
             nc.sync.dma_start(out=out[n, P * s : P * (s + 1)].rearrange("p h c -> p (h c)"), in_=result[:])
 

@@ -24,6 +24,8 @@ N_BANK = 512
 BANKS = CH // N_BANK
 SEQ_TILES = SEQ // P
 TILES = SEQ_TILES * BATCH
+VECTOR_HEADS = 7
+
 FLOPS = 2 * BATCH * SEQ * CH * CH
 
 
@@ -83,7 +85,7 @@ def tile_selfattention_pa_t_kernel(tc, x, freqs, w_words, w_scales, b, g, out):
                 op=ALU.mult,
             )
 
-        xt, grouped, x_codes, x_scales, acc, u_sb, rms, rstd, terms, tab = {}, {}, {}, {}, {}, {}, {}, {}, {}, {}
+        xt, grouped, x_codes, x_scales, acc, u_sb, rstd, terms, tab = {}, {}, {}, {}, {}, {}, {}, {}, {}
 
         def transposes(i):
             x_words = x_sb[i][:].bitcast(F32)
@@ -146,36 +148,39 @@ def tile_selfattention_pa_t_kernel(tc, x, freqs, w_words, w_scales, b, g, out):
                     func=ACT.Square,
                     accum_out=sum_sq[:, h : h + 1],
                 )
-            rms[i] = small.tile([P, HEADS], F32, name="rms")
+            rstd[i] = small.tile([P, HEADS], F32, name="rstd")
             nc.scalar.activation(
-                out=rms[i][:], in_=sum_sq[:], func=ACT.Sqrt, bias=eps_col[:, 0:1], scale=1.0 / HEAD_DIM
+                out=rstd[i][:],
+                in_=sum_sq[:],
+                func=ACT.Abs_reciprocal_sqrt,
+                bias=eps_col[:, 0:1],
+                scale=1.0 / HEAD_DIM,
             )
 
-        def reciprocal(i):
-            rstd[i] = small.tile([P, HEADS], F32, name="rstd")
-            nc.vector.reciprocal(out=rstd[i][:], in_=rms[i][:])
+        def products(engine, i, first_head, heads, table_kji):
+            cols = slice(HEAD_DIM * first_head, HEAD_DIM * (first_head + heads))
+            full = [P, 2, heads, PAIRS, 2]
+            engine.tensor_tensor(
+                out=terms[i][:, :, cols].rearrange("p k (h j i) -> p k h j i", h=heads, j=PAIRS, i=2),
+                in0=u_sb[i][:, cols]
+                .rearrange("p (h j k o) -> p k h j o", h=heads, j=PAIRS, k=2, o=1)
+                .to_broadcast(full),
+                in1=table_kji.rearrange("p (k o j i) -> p k o j i", k=2, o=1, j=PAIRS, i=2).to_broadcast(full),
+                op=ALU.mult,
+            )
 
-        def rotate(i):
-            u_pairs = u_sb[i][:].rearrange("p (h j k) -> p h j k", h=HEADS, j=PAIRS, k=2)
-            full = [P, HEADS, PAIRS, 2]
-            terms[i] = []
-            for k in range(2):
-                term = work.tile([P, CH], F32, name="term%d" % k)
-                nc.vector.tensor_tensor(
-                    out=term[:].rearrange("p (h j i) -> p h j i", h=HEADS, j=PAIRS, i=2),
-                    in0=u_pairs[:, :, :, k : k + 1].to_broadcast(full),
-                    in1=tab[i // BATCH][:, HEAD_DIM * k : HEAD_DIM * (k + 1)]
-                    .rearrange("p (o j i) -> p o j i", o=1, j=PAIRS, i=2)
-                    .to_broadcast(full),
-                    op=ALU.mult,
-                )
-                terms[i].append(term)
+        def products_on_vector(i):
+            terms[i] = work.tile([P, 2, CH], F32, name="terms")
+            products(nc.vector, i, 0, VECTOR_HEADS, tab[i // BATCH][:])
+
+        def products_on_gpsimd(i):
+            products(nc.gpsimd, i, VECTOR_HEADS, HEADS - VECTOR_HEADS, table[:, i // BATCH, :])
 
         def add_terms(i):
-            nc.gpsimd.tensor_tensor(out=terms[i][0][:], in0=terms[i][0][:], in1=terms[i][1][:], op=ALU.add)
+            nc.gpsimd.tensor_tensor(out=terms[i][:, 0, :], in0=terms[i][:, 0, :], in1=terms[i][:, 1, :], op=ALU.add)
 
         def scale_and_store(i):
-            rotated = terms[i][0]
+            rotated = terms[i][:, 0, :]
             result = work.tile([P, CH], F32, name="result")
             for h in range(HEADS):
                 cols = slice(HEAD_DIM * h, HEAD_DIM * (h + 1))
@@ -195,10 +200,10 @@ def tile_selfattention_pa_t_kernel(tc, x, freqs, w_words, w_scales, b, g, out):
                 table_to_psum((step + 1) // BATCH)
             run(transposes, step + 3)
             run(regroup, step + 2)
-            run(rotate, step)
+            run(products_on_vector, step)
             run(quantise, step + 2)
             run(add_bias, step + 1)
             run(statistics, step)
-            run(reciprocal, step)
             run(add_terms, step - 1)
+            run(products_on_gpsimd, step)
             run(scale_and_store, step - 1)

@@ -24,7 +24,9 @@ N_BANK = 512
 BANKS = CH // N_BANK
 SEQ_TILES = SEQ // P
 TILES = SEQ_TILES * BATCH
-VECTOR_HEADS = 7
+VECTOR_HEADS = 6
+TENSOR_COLS = HEAD_DIM * (HEADS - VECTOR_HEADS)
+VECTOR_COLS = HEAD_DIM * VECTOR_HEADS
 
 FLOPS = 2 * BATCH * SEQ * CH * CH
 
@@ -40,7 +42,7 @@ def tile_selfattention_pa_t_kernel(tc, x, freqs, w_words, w_scales, b, g, out):
         small = ctx.enter_context(tc.tile_pool(name="small", bufs=4))
         psum_x = ctx.enter_context(tc.psum_pool(name="psum_x", bufs=2))
         psum_acc = ctx.enter_context(tc.psum_pool(name="psum_acc", bufs=2 * BANKS))
-        psum_tab = ctx.enter_context(tc.psum_pool(name="psum_tab", bufs=2))
+        psum_one = ctx.enter_context(tc.psum_pool(name="psum_one", bufs=1))
 
         def load_x(i):
             x_tile = x_pool.tile([P, CH], BF16, name="x_tile")
@@ -85,6 +87,9 @@ def tile_selfattention_pa_t_kernel(tc, x, freqs, w_words, w_scales, b, g, out):
                 op=ALU.mult,
             )
 
+        tab_bank = psum_one.tile([P, 2, 2 * HEAD_DIM], F32, name="tab_bank")
+        sum_bank = psum_one.tile([P, 2, TENSOR_COLS], F32, name="sum_bank")
+
         xt, grouped, x_codes, x_scales, acc, u_sb, rstd, terms, tab = {}, {}, {}, {}, {}, {}, {}, {}, {}
 
         def transposes(i):
@@ -127,8 +132,8 @@ def tile_selfattention_pa_t_kernel(tc, x, freqs, w_words, w_scales, b, g, out):
                 acc[i].append(acc_bank)
 
         def table_to_psum(s):
-            tab[s] = psum_tab.tile([P, 2 * HEAD_DIM], F32, name="tab")
-            nc.tensor.matmul(out=tab[s][:], lhsT=ident[:], rhs=table[:, s, :], start=True, stop=True)
+            tab[s] = tab_bank[:, s % 2, :]
+            nc.tensor.matmul(out=tab[s], lhsT=ident[:], rhs=table[:, s, :], start=True, stop=True)
 
         def add_bias(i):
             u_sb[i] = work.tile([P, CH], F32, name="u_sb")
@@ -171,21 +176,40 @@ def tile_selfattention_pa_t_kernel(tc, x, freqs, w_words, w_scales, b, g, out):
 
         def products_on_vector(i):
             terms[i] = work.tile([P, 2, CH], F32, name="terms")
-            products(nc.vector, i, 0, VECTOR_HEADS, tab[i // BATCH][:])
+            products(nc.vector, i, 0, VECTOR_HEADS, tab[i // BATCH])
 
         def products_on_gpsimd(i):
             products(nc.gpsimd, i, VECTOR_HEADS, HEADS - VECTOR_HEADS, table[:, i // BATCH, :])
 
         def add_terms(i):
-            nc.gpsimd.tensor_tensor(out=terms[i][:, 0, :], in0=terms[i][:, 0, :], in1=terms[i][:, 1, :], op=ALU.add)
+            nc.gpsimd.tensor_tensor(
+                out=terms[i][:, 0, :VECTOR_COLS],
+                in0=terms[i][:, 0, :VECTOR_COLS],
+                in1=terms[i][:, 1, :VECTOR_COLS],
+                op=ALU.add,
+            )
+
+        def add_terms_on_tensor(i):
+            for k in range(2):
+                nc.tensor.matmul(
+                    out=sum_bank[:, i % 2, :],
+                    lhsT=ident[:],
+                    rhs=terms[i][:, k, VECTOR_COLS:],
+                    start=(k == 0),
+                    stop=(k == 1),
+                )
 
         def scale_and_store(i):
             rotated = terms[i][:, 0, :]
             result = work.tile([P, CH], F32, name="result")
             for h in range(HEADS):
                 cols = slice(HEAD_DIM * h, HEAD_DIM * (h + 1))
+                if h < VECTOR_HEADS:
+                    summed = rotated[:, cols]
+                else:
+                    summed = sum_bank[:, i % 2, HEAD_DIM * (h - VECTOR_HEADS) : HEAD_DIM * (h - VECTOR_HEADS + 1)]
                 nc.scalar.activation(
-                    out=result[:, cols], in_=rotated[:, cols], func=ACT.Copy, scale=rstd[i][:, h : h + 1]
+                    out=result[:, cols], in_=summed, func=ACT.Copy, scale=rstd[i][:, h : h + 1]
                 )
             s, n = divmod(i, BATCH)
             nc.sync.dma_start(out=out[n, P * s : P * (s + 1)].rearrange("p h c -> p (h c)"), in_=result[:])
@@ -198,6 +222,7 @@ def tile_selfattention_pa_t_kernel(tc, x, freqs, w_words, w_scales, b, g, out):
             run(multiply, step + 1)
             if (step + 1) % BATCH == 0 and step + 1 < TILES:
                 table_to_psum((step + 1) // BATCH)
+            run(add_terms_on_tensor, step - 1)
             run(transposes, step + 3)
             run(regroup, step + 2)
             run(products_on_vector, step)

@@ -27,6 +27,7 @@ TILES = SEQ_TILES * BATCH
 VECTOR_HEADS = 6
 TENSOR_COLS = HEAD_DIM * (HEADS - VECTOR_HEADS)
 VECTOR_COLS = HEAD_DIM * VECTOR_HEADS
+LAST_PIECES = [(0, VECTOR_HEADS // 2), (VECTOR_HEADS // 2, VECTOR_HEADS), (VECTOR_HEADS, HEADS)]
 
 FLOPS = 2 * BATCH * SEQ * CH * CH
 
@@ -61,15 +62,20 @@ def tile_selfattention_pa_t_kernel(tc, x, freqs, w_words, w_scales, b, g, out):
             )
         w_sb = const.tile([P, PASSES, 2 * CH], U8, align_bytes=64)
         nc.sync.dma_start(out=w_sb[:].bitcast(I32), in_=w_words.bitcast(I32).rearrange("g p n -> p g n"))
-        for i in range(1, TILES):
-            x_sb.append(load_x(i))
-
-        freqs_sb = const.tile([P, SEQ_TILES, 4 * PAIRS], BF16)
-        nc.scalar.dma_start(out=freqs_sb[:], in_=freqs[0, :, 0].rearrange("(s p) j i k -> p s (j i k)", p=P))
+        x_sb.append(load_x(1))
         gain_bc = const.tile([P, HEAD_DIM], BF16)
-        nc.scalar.dma_start(out=gain_bc[:], in_=g.partition_broadcast(P))
+        nc.sync.dma_start(out=gain_bc[:], in_=g.partition_broadcast(P))
+        freqs_sb = const.tile([P, SEQ_TILES, 4 * PAIRS], BF16)
+        freqs_rows = freqs[0, :, 0].rearrange("(s p) j i k -> p s (j i k)", p=P)
+        half = SEQ_TILES // 2
+        nc.sync.dma_start(out=freqs_sb[:, :half, :], in_=freqs_rows[:, :half, :])
         bias_bc = const.tile([P, CH], BF16)
-        nc.scalar.dma_start(out=bias_bc[:], in_=b.partition_broadcast(P))
+        nc.sync.dma_start(out=bias_bc[:], in_=b.partition_broadcast(P))
+        x_sb.append(load_x(2))
+        x_sb.append(load_x(3))
+        nc.sync.dma_start(out=freqs_sb[:, half:, :], in_=freqs_rows[:, half:, :])
+        for i in range(4, TILES):
+            x_sb.append(load_x(i))
 
         ident = const.tile([P, P], F32)
         make_identity(nc, ident[:])
@@ -77,8 +83,9 @@ def tile_selfattention_pa_t_kernel(tc, x, freqs, w_words, w_scales, b, g, out):
         nc.vector.memset(eps_col[:], EPS)
 
         table = const.tile([P, SEQ_TILES, 2 * HEAD_DIM], F32)
-        for s in range(SEQ_TILES):
-            nc.gpsimd.tensor_tensor(
+
+        def build_table(engine, s):
+            engine.tensor_tensor(
                 out=table[:, s, :].rearrange("p (k j i) -> p k j i", k=2, j=PAIRS, i=2),
                 in0=freqs_sb[:, s, :].rearrange("p (j i k) -> p k j i", j=PAIRS, i=2, k=2),
                 in1=gain_bc[:]
@@ -86,6 +93,9 @@ def tile_selfattention_pa_t_kernel(tc, x, freqs, w_words, w_scales, b, g, out):
                 .to_broadcast([P, 2, PAIRS, 2]),
                 op=ALU.mult,
             )
+
+        for s in range(half):
+            build_table(nc.gpsimd, s)
 
         tab_bank = psum_one.tile([P, 2, 2 * HEAD_DIM], F32, name="tab_bank")
         sum_bank = psum_one.tile([P, 2, TENSOR_COLS], F32, name="sum_bank")
@@ -182,12 +192,15 @@ def tile_selfattention_pa_t_kernel(tc, x, freqs, w_words, w_scales, b, g, out):
             products(nc.gpsimd, i, VECTOR_HEADS, HEADS - VECTOR_HEADS, table[:, i // BATCH, :])
 
         def add_terms(i):
-            nc.gpsimd.tensor_tensor(
-                out=terms[i][:, 0, :VECTOR_COLS],
-                in0=terms[i][:, 0, :VECTOR_COLS],
-                in1=terms[i][:, 1, :VECTOR_COLS],
-                op=ALU.add,
-            )
+            if i < TILES - 1:
+                engine, pieces = nc.gpsimd, [(0, VECTOR_HEADS)]
+            else:
+                engine, pieces = nc.vector, LAST_PIECES
+            for first, last in pieces:
+                cols = slice(HEAD_DIM * first, HEAD_DIM * last)
+                engine.tensor_tensor(
+                    out=terms[i][:, 0, cols], in0=terms[i][:, 0, cols], in1=terms[i][:, 1, cols], op=ALU.add
+                )
 
         def add_terms_on_tensor(i):
             for k in range(2):
@@ -202,17 +215,21 @@ def tile_selfattention_pa_t_kernel(tc, x, freqs, w_words, w_scales, b, g, out):
         def scale_and_store(i):
             rotated = terms[i][:, 0, :]
             result = work.tile([P, CH], F32, name="result")
-            for h in range(HEADS):
-                cols = slice(HEAD_DIM * h, HEAD_DIM * (h + 1))
-                if h < VECTOR_HEADS:
-                    summed = rotated[:, cols]
-                else:
-                    summed = sum_bank[:, i % 2, HEAD_DIM * (h - VECTOR_HEADS) : HEAD_DIM * (h - VECTOR_HEADS + 1)]
-                nc.scalar.activation(
-                    out=result[:, cols], in_=summed, func=ACT.Copy, scale=rstd[i][:, h : h + 1]
-                )
             s, n = divmod(i, BATCH)
-            nc.sync.dma_start(out=out[n, P * s : P * (s + 1)].rearrange("p h c -> p (h c)"), in_=result[:])
+            for first, last in [(0, HEADS)] if i < TILES - 1 else LAST_PIECES:
+                for h in range(first, last):
+                    cols = slice(HEAD_DIM * h, HEAD_DIM * (h + 1))
+                    if h < VECTOR_HEADS or i == TILES - 1:
+                        summed = rotated[:, cols]
+                    else:
+                        summed = sum_bank[:, i % 2, HEAD_DIM * (h - VECTOR_HEADS) : HEAD_DIM * (h - VECTOR_HEADS + 1)]
+                    nc.scalar.activation(
+                        out=result[:, cols], in_=summed, func=ACT.Copy, scale=rstd[i][:, h : h + 1]
+                    )
+                nc.sync.dma_start(
+                    out=out[n, P * s : P * (s + 1), first:last, :].rearrange("p h c -> p (h c)"),
+                    in_=result[:, HEAD_DIM * first : HEAD_DIM * last],
+                )
 
         def run(stage, i):
             if 0 <= i < TILES:
@@ -222,12 +239,15 @@ def tile_selfattention_pa_t_kernel(tc, x, freqs, w_words, w_scales, b, g, out):
             run(multiply, step + 1)
             if (step + 1) % BATCH == 0 and step + 1 < TILES:
                 table_to_psum((step + 1) // BATCH)
-            run(add_terms_on_tensor, step - 1)
+            if step < TILES:
+                run(add_terms_on_tensor, step - 1)
             run(transposes, step + 3)
             run(regroup, step + 2)
             run(products_on_vector, step)
             run(quantise, step + 2)
             run(add_bias, step + 1)
+            if 1 <= step <= half:
+                build_table(nc.vector, half + step - 1)
             run(statistics, step)
             run(add_terms, step - 1)
             run(products_on_gpsimd, step)

@@ -217,7 +217,7 @@ def tile_selfattention_pa_t_kernel(tc, x, freqs, w_words, w_scales, b, g, out):
             result = work.tile([P, CH], F32, name="result")
             s, n = divmod(i, BATCH)
             for first, last in [(0, HEADS)] if i < TILES - 1 else LAST_PIECES:
-                for h in range(first, last):
+                for h in reversed(range(first, last)):
                     cols = slice(HEAD_DIM * h, HEAD_DIM * (h + 1))
                     if h < VECTOR_HEADS or i == TILES - 1:
                         summed = rotated[:, cols]
@@ -237,13 +237,13 @@ def tile_selfattention_pa_t_kernel(tc, x, freqs, w_words, w_scales, b, g, out):
 
         for step in range(-3, TILES + 1):
             run(multiply, step + 1)
-            if (step + 1) % BATCH == 0 and step + 1 < TILES:
-                table_to_psum((step + 1) // BATCH)
             if step < TILES:
                 run(add_terms_on_tensor, step - 1)
             run(transposes, step + 3)
             run(regroup, step + 2)
             run(products_on_vector, step)
+            if (step + 1) % BATCH == 0 and step + 1 < TILES:
+                table_to_psum((step + 1) // BATCH)
             run(quantise, step + 2)
             run(add_bias, step + 1)
             if 1 <= step <= half:

@@ -38,9 +38,10 @@ def tile_selfattention_pa_t_kernel(tc, x, freqs, w_words, w_scales, b, g, out):
         ctx.enter_context(tc.manual_schedule())
         const = ctx.enter_context(tc.tile_pool(name="const", bufs=1))
         x_pool = ctx.enter_context(tc.tile_pool(name="x_pool", bufs=TILES))
-        quant = ctx.enter_context(tc.tile_pool(name="quant", bufs=3))
-        work = ctx.enter_context(tc.tile_pool(name="work", bufs=3))
-        small = ctx.enter_context(tc.tile_pool(name="small", bufs=4))
+        quant = ctx.enter_context(tc.tile_pool(name="quant", bufs=4))
+        work = ctx.enter_context(tc.tile_pool(name="work", bufs=4))
+        stored = ctx.enter_context(tc.tile_pool(name="stored", bufs=8))
+        small = ctx.enter_context(tc.tile_pool(name="small", bufs=8))
         psum_x = ctx.enter_context(tc.psum_pool(name="psum_x", bufs=2))
         psum_acc = ctx.enter_context(tc.psum_pool(name="psum_acc", bufs=2 * BANKS))
         psum_one = ctx.enter_context(tc.psum_pool(name="psum_one", bufs=1))
@@ -113,7 +114,8 @@ def tile_selfattention_pa_t_kernel(tc, x, freqs, w_words, w_scales, b, g, out):
 
         def regroup(i):
             grouped[i] = quant.tile([P, PASSES * P * 4], BF16, align_bytes=64, name="grouped")
-            nc.scalar.copy(
+            copy = nc.vector.tensor_copy if i % 3 == 0 else nc.scalar.copy
+            copy(
                 out=grouped[i][:].bitcast(F32).rearrange("p (g r u) -> p g r u", g=PASSES, r=P, u=2),
                 in_=xt[i][:].rearrange("p g u r -> p g r u"),
             )
@@ -214,7 +216,7 @@ def tile_selfattention_pa_t_kernel(tc, x, freqs, w_words, w_scales, b, g, out):
 
         def scale_and_store(i):
             rotated = terms[i][:, 0, :]
-            result = work.tile([P, CH], F32, name="result")
+            result = stored.tile([P, CH], F32, name="result")
             s, n = divmod(i, BATCH)
             for first, last in [(0, HEADS)] if i < TILES - 1 else LAST_PIECES:
                 for h in reversed(range(first, last)):

@@ -38,8 +38,8 @@ def tile_selfattention_pa_t_kernel(tc, x, freqs, w_words, w_scales, b, g, out):
         ctx.enter_context(tc.manual_schedule())
         const = ctx.enter_context(tc.tile_pool(name="const", bufs=1))
         x_pool = ctx.enter_context(tc.tile_pool(name="x_pool", bufs=TILES))
-        quant = ctx.enter_context(tc.tile_pool(name="quant", bufs=4))
-        work = ctx.enter_context(tc.tile_pool(name="work", bufs=4))
+        quant = ctx.enter_context(tc.tile_pool(name="quant", bufs=6))
+        work = ctx.enter_context(tc.tile_pool(name="work", bufs=6))
         stored = ctx.enter_context(tc.tile_pool(name="stored", bufs=8))
         small = ctx.enter_context(tc.tile_pool(name="small", bufs=8))
         psum_x = ctx.enter_context(tc.psum_pool(name="psum_x", bufs=2))
@@ -114,7 +114,7 @@ def tile_selfattention_pa_t_kernel(tc, x, freqs, w_words, w_scales, b, g, out):
 
         def regroup(i):
             grouped[i] = quant.tile([P, PASSES * P * 4], BF16, align_bytes=64, name="grouped")
-            copy = nc.vector.tensor_copy if i % 3 == 0 else nc.scalar.copy
+            copy = nc.vector.tensor_copy if i % 4 == 0 else nc.scalar.copy
             copy(
                 out=grouped[i][:].bitcast(F32).rearrange("p (g r u) -> p g r u", g=PASSES, r=P, u=2),
                 in_=xt[i][:].rearrange("p g u r -> p g r u"),
@@ -218,7 +218,13 @@ def tile_selfattention_pa_t_kernel(tc, x, freqs, w_words, w_scales, b, g, out):
             rotated = terms[i][:, 0, :]
             result = stored.tile([P, CH], F32, name="result")
             s, n = divmod(i, BATCH)
-            for first, last in [(0, HEADS)] if i < TILES - 1 else LAST_PIECES:
+            if i < TILES - 3:
+                pieces = [(0, HEADS)]
+            elif i < TILES - 1:
+                pieces = list(reversed(LAST_PIECES))
+            else:
+                pieces = LAST_PIECES
+            for first, last in pieces:
                 for h in reversed(range(first, last)):
                     cols = slice(HEAD_DIM * h, HEAD_DIM * (h + 1))
                     if h < VECTOR_HEADS or i == TILES - 1:

@@ -187,10 +187,10 @@ def tile_selfattention_pa_t_kernel(tc, x, freqs, w_words, w_scales, b, g, out):
             )
 
         def products_on_vector(i):
-            terms[i] = work.tile([P, 2, CH], F32, name="terms")
             products(nc.vector, i, 0, VECTOR_HEADS, tab[i // BATCH])
 
         def products_on_gpsimd(i):
+            terms[i] = work.tile([P, 2, CH], F32, name="terms")
             products(nc.gpsimd, i, VECTOR_HEADS, HEADS - VECTOR_HEADS, table[:, i // BATCH, :])
 
         def add_terms(i):
@@ -252,11 +252,11 @@ def tile_selfattention_pa_t_kernel(tc, x, freqs, w_words, w_scales, b, g, out):
             run(products_on_vector, step)
             if (step + 1) % BATCH == 0 and step + 1 < TILES:
                 table_to_psum((step + 1) // BATCH)
-            run(quantise, step + 2)
             run(add_bias, step + 1)
+            run(quantise, step + 2)
             if 1 <= step <= half:
                 build_table(nc.vector, half + step - 1)
             run(statistics, step)
-            run(add_terms, step - 1)
-            run(products_on_gpsimd, step)
+            run(products_on_gpsimd, step + 1)
+            run(add_terms, step)
             run(scale_and_store, step - 1)

@@ -63,16 +63,17 @@ def tile_selfattention_pa_t_kernel(tc, x, freqs, w_words, w_scales, b, g, out):
             )
         w_sb = const.tile([P, PASSES, 2 * CH], U8, align_bytes=64)
         nc.sync.dma_start(out=w_sb[:].bitcast(I32), in_=w_words.bitcast(I32).rearrange("g p n -> p g n"))
-        x_sb.append(load_x(1))
-        gain_bc = const.tile([P, HEAD_DIM], BF16)
-        nc.sync.dma_start(out=gain_bc[:], in_=g.partition_broadcast(P))
+        row = const.tile([P, CH + HEAD_DIM], BF16)
+        nc.vector.memset(row[:], 0.0)
+        nc.sync.dma_start(out=row[0:1, :CH], in_=b.unsqueeze(0))
+        nc.sync.dma_start(out=row[0:1, CH:], in_=g.unsqueeze(0))
         freqs_sb = const.tile([P, SEQ_TILES, 4 * PAIRS], BF16)
         freqs_rows = freqs[0, :, 0].rearrange("(s p) j i k -> p s (j i k)", p=P)
         half = SEQ_TILES // 2
-        nc.sync.dma_start(out=freqs_sb[:, :half, :], in_=freqs_rows[:, :half, :])
-        bias_bc = const.tile([P, CH], BF16)
-        nc.sync.dma_start(out=bias_bc[:], in_=b.partition_broadcast(P))
+        nc.sync.dma_start(out=freqs_sb[:, :1, :], in_=freqs_rows[:, :1, :])
+        x_sb.append(load_x(1))
         x_sb.append(load_x(2))
+        nc.sync.dma_start(out=freqs_sb[:, 1:half, :], in_=freqs_rows[:, 1:half, :])
         x_sb.append(load_x(3))
         nc.sync.dma_start(out=freqs_sb[:, half:, :], in_=freqs_rows[:, half:, :])
         for i in range(4, TILES):
@@ -80,6 +81,8 @@ def tile_selfattention_pa_t_kernel(tc, x, freqs, w_words, w_scales, b, g, out):
 
         ident = const.tile([P, P], F32)
         make_identity(nc, ident[:])
+        ones = const.tile([P, P], BF16)
+        nc.gpsimd.memset(ones[:], 1.0)
         eps_col = const.tile([P, 1], F32)
         nc.vector.memset(eps_col[:], EPS)
 
@@ -95,8 +98,17 @@ def tile_selfattention_pa_t_kernel(tc, x, freqs, w_words, w_scales, b, g, out):
                 op=ALU.mult,
             )
 
-        for s in range(half):
-            build_table(nc.gpsimd, s)
+        gain_bc = const.tile([P, HEAD_DIM], BF16)
+        bias_bc = const.tile([P, CH], BF16)
+
+        def spread_constants():
+            for tile, first, width in ((gain_bc, CH, HEAD_DIM), (bias_bc, 0, N_BANK), (bias_bc, N_BANK, N_BANK)):
+                spread = psum_acc.tile([P, N_BANK], F32, name="acc_bank")
+                nc.tensor.matmul(
+                    out=spread[:, :width], lhsT=ones[:], rhs=row[:, first : first + width], start=True, stop=True
+                )
+                to = first % CH
+                nc.scalar.copy(out=tile[:, to : to + width], in_=spread[:, :width])
 
         tab_bank = psum_one.tile([P, 2, 2 * HEAD_DIM], F32, name="tab_bank")
         sum_bank = psum_one.tile([P, 2, TENSOR_COLS], F32, name="sum_bank")
@@ -249,11 +261,17 @@ def tile_selfattention_pa_t_kernel(tc, x, freqs, w_words, w_scales, b, g, out):
                 run(add_terms_on_tensor, step - 1)
             run(transposes, step + 3)
             run(regroup, step + 2)
+            if step == -3:
+                spread_constants()
             run(products_on_vector, step)
             if (step + 1) % BATCH == 0 and step + 1 < TILES:
                 table_to_psum((step + 1) // BATCH)
             run(add_bias, step + 1)
             run(quantise, step + 2)
+            if step == -2:
+                build_table(nc.vector, 0)
+                for s in range(1, half):
+                    build_table(nc.gpsimd, s)
             if 1 <= step <= half:
                 build_table(nc.vector, half + step - 1)
             run(statistics, step)

@@ -113,7 +113,7 @@ def tile_selfattention_pa_t_kernel(tc, x, freqs, w_words, w_scales, b, g, out):
         tab_bank = psum_one.tile([P, 2, 2 * HEAD_DIM], F32, name="tab_bank")
         sum_bank = psum_one.tile([P, 2, TENSOR_COLS], F32, name="sum_bank")
 
-        xt, grouped, x_codes, x_scales, acc, u_sb, rstd, terms, tab = {}, {}, {}, {}, {}, {}, {}, {}, {}
+        xt, grouped, x_codes, x_scales, acc, u_sb, rstd, terms, tab, result = {}, {}, {}, {}, {}, {}, {}, {}, {}, {}
 
         def transposes(i):
             x_words = x_sb[i][:].bitcast(F32)
@@ -126,7 +126,7 @@ def tile_selfattention_pa_t_kernel(tc, x, freqs, w_words, w_scales, b, g, out):
 
         def regroup(i):
             grouped[i] = quant.tile([P, PASSES * P * 4], BF16, align_bytes=64, name="grouped")
-            copy = nc.vector.tensor_copy if i % 4 == 0 else nc.scalar.copy
+            copy = nc.vector.tensor_copy if i == 0 else nc.scalar.copy
             copy(
                 out=grouped[i][:].bitcast(F32).rearrange("p (g r u) -> p g r u", g=PASSES, r=P, u=2),
                 in_=xt[i][:].rearrange("p g u r -> p g r u"),
@@ -226,9 +226,20 @@ def tile_selfattention_pa_t_kernel(tc, x, freqs, w_words, w_scales, b, g, out):
                     stop=(k == 1),
                 )
 
+        def scale_on_vector(i):
+            result[i] = stored.tile([P, CH], F32, name="result")
+            heads = HEADS - VECTOR_HEADS
+            nc.vector.tensor_tensor(
+                out=result[i][:, VECTOR_COLS:].rearrange("p (h c) -> p h c", h=heads),
+                in0=sum_bank[:, i % 2, :].rearrange("p (h c) -> p h c", h=heads),
+                in1=rstd[i][:, VECTOR_HEADS:].unsqueeze(2).to_broadcast([P, heads, HEAD_DIM]),
+                op=ALU.mult,
+            )
+
         def scale_and_store(i):
             rotated = terms[i][:, 0, :]
-            result = stored.tile([P, CH], F32, name="result")
+            if i == TILES - 1:
+                result[i] = stored.tile([P, CH], F32, name="result")
             s, n = divmod(i, BATCH)
             if i < TILES - 3:
                 pieces = [(0, HEADS)]
@@ -237,18 +248,14 @@ def tile_selfattention_pa_t_kernel(tc, x, freqs, w_words, w_scales, b, g, out):
             else:
                 pieces = LAST_PIECES
             for first, last in pieces:
-                for h in reversed(range(first, last)):
+                for h in range(first, last if i == TILES - 1 else min(last, VECTOR_HEADS)):
                     cols = slice(HEAD_DIM * h, HEAD_DIM * (h + 1))
-                    if h < VECTOR_HEADS or i == TILES - 1:
-                        summed = rotated[:, cols]
-                    else:
-                        summed = sum_bank[:, i % 2, HEAD_DIM * (h - VECTOR_HEADS) : HEAD_DIM * (h - VECTOR_HEADS + 1)]
                     nc.scalar.activation(
-                        out=result[:, cols], in_=summed, func=ACT.Copy, scale=rstd[i][:, h : h + 1]
+                        out=result[i][:, cols], in_=rotated[:, cols], func=ACT.Copy, scale=rstd[i][:, h : h + 1]
                     )
                 nc.sync.dma_start(
                     out=out[n, P * s : P * (s + 1), first:last, :].rearrange("p h c -> p (h c)"),
-                    in_=result[:, HEAD_DIM * first : HEAD_DIM * last],
+                    in_=result[i][:, HEAD_DIM * first : HEAD_DIM * last],
                 )
 
         def run(stage, i):
@@ -256,14 +263,16 @@ def tile_selfattention_pa_t_kernel(tc, x, freqs, w_words, w_scales, b, g, out):
                 stage(i)
 
         for step in range(-3, TILES + 1):
-            run(multiply, step + 1)
             if step < TILES:
                 run(add_terms_on_tensor, step - 1)
+            run(multiply, step + 1)
             run(transposes, step + 3)
             run(regroup, step + 2)
             if step == -3:
                 spread_constants()
             run(products_on_vector, step)
+            if step < TILES:
+                run(scale_on_vector, step - 1)
             if (step + 1) % BATCH == 0 and step + 1 < TILES:
                 table_to_psum((step + 1) // BATCH)
             run(add_bias, step + 1)

@@ -29,6 +29,8 @@ TENSOR_COLS = HEAD_DIM * (HEADS - VECTOR_HEADS)
 VECTOR_COLS = HEAD_DIM * VECTOR_HEADS
 LAST_PIECES = [(0, VECTOR_HEADS // 2), (VECTOR_HEADS // 2, VECTOR_HEADS), (VECTOR_HEADS, HEADS)]
 
+WARM_UP = 6
+
 FLOPS = 2 * BATCH * SEQ * CH * CH
 
 
@@ -52,6 +54,12 @@ def tile_selfattention_pa_t_kernel(tc, x, freqs, w_words, w_scales, b, g, out):
             nc.sync.dma_start(out=x_tile[:], in_=x[n, P * s : P * (s + 1), :])
             return x_tile
 
+        zeros = const.tile([P, N_BANK], BF16)
+        nc.gpsimd.memset(zeros[:].bitcast(I32), 0)
+        for i in range(WARM_UP):
+            warm = psum_acc.tile([P, N_BANK], F32, name="acc_bank")
+            nc.tensor.matmul(out=warm[:], lhsT=zeros[:, :P], rhs=zeros[:], start=True, stop=True)
+
         x_sb = [load_x(0)]
         w_planes = const.tile([P, PASSES, CH], U8, align_bytes=64)
         nc.vector.memset(w_planes[:].rearrange("p g n -> p (g n)").bitcast(I32), 0)
@@ -61,17 +69,17 @@ def tile_selfattention_pa_t_kernel(tc, x, freqs, w_words, w_scales, b, g, out):
                 out=w_planes[32 * quadrant : 32 * quadrant + 4, :, :].bitcast(I32),
                 in_=scale_rows[:, 4 * quadrant : 4 * quadrant + 4, :].rearrange("g r n -> r g n"),
             )
-        w_sb = const.tile([P, PASSES, 2 * CH], U8, align_bytes=64)
-        nc.sync.dma_start(out=w_sb[:].bitcast(I32), in_=w_words.bitcast(I32).rearrange("g p n -> p g n"))
         row = const.tile([P, CH + HEAD_DIM], BF16)
-        nc.vector.memset(row[:], 0.0)
+        nc.vector.memset(row[:].bitcast(I32), 0)
         nc.sync.dma_start(out=row[0:1, :CH], in_=b.unsqueeze(0))
         nc.sync.dma_start(out=row[0:1, CH:], in_=g.unsqueeze(0))
+        x_sb.append(load_x(1))
+        w_sb = const.tile([P, PASSES, 2 * CH], U8, align_bytes=64)
+        nc.sync.dma_start(out=w_sb[:].bitcast(I32), in_=w_words.bitcast(I32).rearrange("g p n -> p g n"))
         freqs_sb = const.tile([P, SEQ_TILES, 4 * PAIRS], BF16)
         freqs_rows = freqs[0, :, 0].rearrange("(s p) j i k -> p s (j i k)", p=P)
         half = SEQ_TILES // 2
         nc.sync.dma_start(out=freqs_sb[:, :1, :], in_=freqs_rows[:, :1, :])
-        x_sb.append(load_x(1))
         x_sb.append(load_x(2))
         nc.sync.dma_start(out=freqs_sb[:, 1:half, :], in_=freqs_rows[:, 1:half, :])
         x_sb.append(load_x(3))
@@ -209,7 +217,7 @@ def tile_selfattention_pa_t_kernel(tc, x, freqs, w_words, w_scales, b, g, out):
             if i < TILES - 1:
                 engine, pieces = nc.gpsimd, [(0, VECTOR_HEADS)]
             else:
-                engine, pieces = nc.vector, LAST_PIECES
+                engine, pieces = nc.vector, LAST_PIECES[:2]
             for first, last in pieces:
                 cols = slice(HEAD_DIM * first, HEAD_DIM * last)
                 engine.tensor_tensor(
@@ -238,8 +246,6 @@ def tile_selfattention_pa_t_kernel(tc, x, freqs, w_words, w_scales, b, g, out):
 
         def scale_and_store(i):
             rotated = terms[i][:, 0, :]
-            if i == TILES - 1:
-                result[i] = stored.tile([P, CH], F32, name="result")
             s, n = divmod(i, BATCH)
             if i < TILES - 3:
                 pieces = [(0, HEADS)]
@@ -248,11 +254,17 @@ def tile_selfattention_pa_t_kernel(tc, x, freqs, w_words, w_scales, b, g, out):
             else:
                 pieces = LAST_PIECES
             for first, last in pieces:
-                for h in range(first, last if i == TILES - 1 else min(last, VECTOR_HEADS)):
+                for h in range(first, min(last, VECTOR_HEADS)):
                     cols = slice(HEAD_DIM * h, HEAD_DIM * (h + 1))
-                    nc.scalar.activation(
-                        out=result[i][:, cols], in_=rotated[:, cols], func=ACT.Copy, scale=rstd[i][:, h : h + 1]
-                    )
+                    factor = rstd[i][:, h : h + 1]
+                    if i == TILES - 1 and h >= VECTOR_HEADS - 2:
+                        nc.vector.tensor_scalar(
+                            out=result[i][:, cols], in0=rotated[:, cols], scalar1=factor, scalar2=None, op0=ALU.mult
+                        )
+                    else:
+                        nc.scalar.activation(
+                            out=result[i][:, cols], in_=rotated[:, cols], func=ACT.Copy, scale=factor
+                        )
                 nc.sync.dma_start(
                     out=out[n, P * s : P * (s + 1), first:last, :].rearrange("p h c -> p (h c)"),
                     in_=result[i][:, HEAD_DIM * first : HEAD_DIM * last],
@@ -263,16 +275,14 @@ def tile_selfattention_pa_t_kernel(tc, x, freqs, w_words, w_scales, b, g, out):
                 stage(i)
 
         for step in range(-3, TILES + 1):
-            if step < TILES:
-                run(add_terms_on_tensor, step - 1)
+            run(add_terms_on_tensor, step - 1)
             run(multiply, step + 1)
             run(transposes, step + 3)
             run(regroup, step + 2)
-            if step == -3:
+            if step == -2:
                 spread_constants()
             run(products_on_vector, step)
-            if step < TILES:
-                run(scale_on_vector, step - 1)
+            run(scale_on_vector, step - 1)
             if (step + 1) % BATCH == 0 and step + 1 < TILES:
                 table_to_psum((step + 1) // BATCH)
             run(add_bias, step + 1)

@@ -29,7 +29,7 @@ TENSOR_COLS = HEAD_DIM * (HEADS - VECTOR_HEADS)
 VECTOR_COLS = HEAD_DIM * VECTOR_HEADS
 LAST_PIECES = [(0, VECTOR_HEADS // 2), (VECTOR_HEADS // 2, VECTOR_HEADS), (VECTOR_HEADS, HEADS)]
 
-WARM_UP = 6
+WARM_UP = 4
 
 FLOPS = 2 * BATCH * SEQ * CH * CH
 
@@ -61,6 +61,10 @@ def tile_selfattention_pa_t_kernel(tc, x, freqs, w_words, w_scales, b, g, out):
             nc.tensor.matmul(out=warm[:], lhsT=zeros[:, :P], rhs=zeros[:], start=True, stop=True)
 
         x_sb = [load_x(0)]
+        row = const.tile([P, CH + HEAD_DIM], BF16)
+        nc.vector.memset(row[:].bitcast(I32), 0)
+        nc.sync.dma_start(out=row[0:1, :CH], in_=b.unsqueeze(0))
+        nc.sync.dma_start(out=row[0:1, CH:], in_=g.unsqueeze(0))
         w_planes = const.tile([P, PASSES, CH], U8, align_bytes=64)
         nc.vector.memset(w_planes[:].rearrange("p g n -> p (g n)").bitcast(I32), 0)
         scale_rows = w_scales.bitcast(I32)
@@ -69,17 +73,13 @@ def tile_selfattention_pa_t_kernel(tc, x, freqs, w_words, w_scales, b, g, out):
                 out=w_planes[32 * quadrant : 32 * quadrant + 4, :, :].bitcast(I32),
                 in_=scale_rows[:, 4 * quadrant : 4 * quadrant + 4, :].rearrange("g r n -> r g n"),
             )
-        row = const.tile([P, CH + HEAD_DIM], BF16)
-        nc.vector.memset(row[:].bitcast(I32), 0)
-        nc.sync.dma_start(out=row[0:1, :CH], in_=b.unsqueeze(0))
-        nc.sync.dma_start(out=row[0:1, CH:], in_=g.unsqueeze(0))
-        x_sb.append(load_x(1))
         w_sb = const.tile([P, PASSES, 2 * CH], U8, align_bytes=64)
         nc.sync.dma_start(out=w_sb[:].bitcast(I32), in_=w_words.bitcast(I32).rearrange("g p n -> p g n"))
         freqs_sb = const.tile([P, SEQ_TILES, 4 * PAIRS], BF16)
         freqs_rows = freqs[0, :, 0].rearrange("(s p) j i k -> p s (j i k)", p=P)
         half = SEQ_TILES // 2
         nc.sync.dma_start(out=freqs_sb[:, :1, :], in_=freqs_rows[:, :1, :])
+        x_sb.append(load_x(1))
         x_sb.append(load_x(2))
         nc.sync.dma_start(out=freqs_sb[:, 1:half, :], in_=freqs_rows[:, 1:half, :])
         x_sb.append(load_x(3))
@@ -90,7 +90,7 @@ def tile_selfattention_pa_t_kernel(tc, x, freqs, w_words, w_scales, b, g, out):
         ident = const.tile([P, P], F32)
         make_identity(nc, ident[:])
         ones = const.tile([P, P], BF16)
-        nc.gpsimd.memset(ones[:], 1.0)
+        nc.vector.memset(ones[:], 1.0)
         eps_col = const.tile([P, 1], F32)
         nc.vector.memset(eps_col[:], EPS)
 
@@ -121,7 +121,7 @@ def tile_selfattention_pa_t_kernel(tc, x, freqs, w_words, w_scales, b, g, out):
         tab_bank = psum_one.tile([P, 2, 2 * HEAD_DIM], F32, name="tab_bank")
         sum_bank = psum_one.tile([P, 2, TENSOR_COLS], F32, name="sum_bank")
 
-        xt, grouped, x_codes, x_scales, acc, u_sb, rstd, terms, tab, result = {}, {}, {}, {}, {}, {}, {}, {}, {}, {}
+        xt, grouped, x_codes, x_scales, acc, u_sb, rstd, terms, tensor_terms, tab, sums, result = {}, {}, {}, {}, {}, {}, {}, {}, {}, {}, {}, {}
 
         def transposes(i):
             x_words = x_sb[i][:].bitcast(F32)
@@ -194,11 +194,11 @@ def tile_selfattention_pa_t_kernel(tc, x, freqs, w_words, w_scales, b, g, out):
                 scale=1.0 / HEAD_DIM,
             )
 
-        def products(engine, i, first_head, heads, table_kji):
+        def products(engine, dest, i, first_head, heads, table_kji):
             cols = slice(HEAD_DIM * first_head, HEAD_DIM * (first_head + heads))
             full = [P, 2, heads, PAIRS, 2]
             engine.tensor_tensor(
-                out=terms[i][:, :, cols].rearrange("p k (h j i) -> p k h j i", h=heads, j=PAIRS, i=2),
+                out=dest[:].rearrange("p k (h j i) -> p k h j i", h=heads, j=PAIRS, i=2),
                 in0=u_sb[i][:, cols]
                 .rearrange("p (h j k o) -> p k h j o", h=heads, j=PAIRS, k=2, o=1)
                 .to_broadcast(full),
@@ -207,11 +207,12 @@ def tile_selfattention_pa_t_kernel(tc, x, freqs, w_words, w_scales, b, g, out):
             )
 
         def products_on_vector(i):
-            products(nc.vector, i, 0, VECTOR_HEADS, tab[i // BATCH])
+            terms[i] = work.tile([P, 2, VECTOR_COLS], F32, name="terms")
+            products(nc.vector, terms[i], i, 0, VECTOR_HEADS, tab[i // BATCH])
 
         def products_on_gpsimd(i):
-            terms[i] = work.tile([P, 2, CH], F32, name="terms")
-            products(nc.gpsimd, i, VECTOR_HEADS, HEADS - VECTOR_HEADS, table[:, i // BATCH, :])
+            tensor_terms[i] = work.tile([P, 2, TENSOR_COLS], F32, name="tensor_terms")
+            products(nc.gpsimd, tensor_terms[i], i, VECTOR_HEADS, HEADS - VECTOR_HEADS, table[:, i // BATCH, :])
 
         def add_terms(i):
             if i < TILES - 1:
@@ -225,11 +226,16 @@ def tile_selfattention_pa_t_kernel(tc, x, freqs, w_words, w_scales, b, g, out):
                 )
 
         def add_terms_on_tensor(i):
+            if i < TILES - 1:
+                sums[i] = sum_bank[:, i % 2, :]
+            else:
+                last_sums = psum_acc.tile([P, N_BANK], F32, name="acc_bank")
+                sums[i] = last_sums[:, :TENSOR_COLS]
             for k in range(2):
                 nc.tensor.matmul(
-                    out=sum_bank[:, i % 2, :],
+                    out=sums[i],
                     lhsT=ident[:],
-                    rhs=terms[i][:, k, VECTOR_COLS:],
+                    rhs=tensor_terms[i][:, k, :],
                     start=(k == 0),
                     stop=(k == 1),
                 )
@@ -239,7 +245,7 @@ def tile_selfattention_pa_t_kernel(tc, x, freqs, w_words, w_scales, b, g, out):
             heads = HEADS - VECTOR_HEADS
             nc.vector.tensor_tensor(
                 out=result[i][:, VECTOR_COLS:].rearrange("p (h c) -> p h c", h=heads),
-                in0=sum_bank[:, i % 2, :].rearrange("p (h c) -> p h c", h=heads),
+                in0=sums[i].rearrange("p (h c) -> p h c", h=heads),
                 in1=rstd[i][:, VECTOR_HEADS:].unsqueeze(2).to_broadcast([P, heads, HEAD_DIM]),
                 op=ALU.mult,
             )
@@ -277,10 +283,11 @@ def tile_selfattention_pa_t_kernel(tc, x, freqs, w_words, w_scales, b, g, out):
         for step in range(-3, TILES + 1):
             run(add_terms_on_tensor, step - 1)
             run(multiply, step + 1)
-            run(transposes, step + 3)
-            run(regroup, step + 2)
-            if step == -2:
+            for i in {-2: (), -1: (1, 2)}.get(step, (step + 3,)):
+                run(transposes, i)
+            if step == -3:
                 spread_constants()
+            run(regroup, step + 2)
             run(products_on_vector, step)
             run(scale_on_vector, step - 1)
             if (step + 1) % BATCH == 0 and step + 1 < TILES:

@@ -121,7 +121,7 @@ def tile_selfattention_pa_t_kernel(tc, x, freqs, w_words, w_scales, b, g, out):
         tab_bank = psum_one.tile([P, 2, 2 * HEAD_DIM], F32, name="tab_bank")
         sum_bank = psum_one.tile([P, 2, TENSOR_COLS], F32, name="sum_bank")
 
-        xt, grouped, x_codes, x_scales, acc, u_sb, rstd, terms, tensor_terms, tab, sums, result = {}, {}, {}, {}, {}, {}, {}, {}, {}, {}, {}, {}
+        xt, grouped, x_codes, x_scales, acc, u_sb, rstd, terms, tensor_terms, tab, result = {}, {}, {}, {}, {}, {}, {}, {}, {}, {}, {}
 
         def transposes(i):
             x_words = x_sb[i][:].bitcast(F32)
@@ -207,6 +207,8 @@ def tile_selfattention_pa_t_kernel(tc, x, freqs, w_words, w_scales, b, g, out):
             )
 
         def products_on_vector(i):
+            if i == TILES - 1:
+                tensor_terms[i] = work.tile([P, 2, TENSOR_COLS], F32, name="tensor_terms")
             terms[i] = work.tile([P, 2, VECTOR_COLS], F32, name="terms")
             products(nc.vector, terms[i], i, 0, VECTOR_HEADS, tab[i // BATCH])
 
@@ -215,25 +217,12 @@ def tile_selfattention_pa_t_kernel(tc, x, freqs, w_words, w_scales, b, g, out):
             products(nc.gpsimd, tensor_terms[i], i, VECTOR_HEADS, HEADS - VECTOR_HEADS, table[:, i // BATCH, :])
 
         def add_terms(i):
-            if i < TILES - 1:
-                engine, pieces = nc.gpsimd, [(0, VECTOR_HEADS)]
-            else:
-                engine, pieces = nc.vector, LAST_PIECES[:2]
-            for first, last in pieces:
-                cols = slice(HEAD_DIM * first, HEAD_DIM * last)
-                engine.tensor_tensor(
-                    out=terms[i][:, 0, cols], in0=terms[i][:, 0, cols], in1=terms[i][:, 1, cols], op=ALU.add
-                )
+            nc.gpsimd.tensor_tensor(out=terms[i][:, 0, :], in0=terms[i][:, 0, :], in1=terms[i][:, 1, :], op=ALU.add)
 
         def add_terms_on_tensor(i):
-            if i < TILES - 1:
-                sums[i] = sum_bank[:, i % 2, :]
-            else:
-                last_sums = psum_acc.tile([P, N_BANK], F32, name="acc_bank")
-                sums[i] = last_sums[:, :TENSOR_COLS]
             for k in range(2):
                 nc.tensor.matmul(
-                    out=sums[i],
+                    out=sum_bank[:, i % 2, :],
                     lhsT=ident[:],
                     rhs=tensor_terms[i][:, k, :],
                     start=(k == 0),
@@ -245,42 +234,55 @@ def tile_selfattention_pa_t_kernel(tc, x, freqs, w_words, w_scales, b, g, out):
             heads = HEADS - VECTOR_HEADS
             nc.vector.tensor_tensor(
                 out=result[i][:, VECTOR_COLS:].rearrange("p (h c) -> p h c", h=heads),
-                in0=sums[i].rearrange("p (h c) -> p h c", h=heads),
+                in0=sum_bank[:, i % 2, :].rearrange("p (h c) -> p h c", h=heads),
                 in1=rstd[i][:, VECTOR_HEADS:].unsqueeze(2).to_broadcast([P, heads, HEAD_DIM]),
                 op=ALU.mult,
             )
 
         def scale_and_store(i):
-            rotated = terms[i][:, 0, :]
-            s, n = divmod(i, BATCH)
-            if i < TILES - 3:
-                pieces = [(0, HEADS)]
-            elif i < TILES - 1:
-                pieces = list(reversed(LAST_PIECES))
-            else:
-                pieces = LAST_PIECES
+            pieces = [(0, HEADS)] if i < TILES - 3 else list(reversed(LAST_PIECES))
             for first, last in pieces:
                 for h in range(first, min(last, VECTOR_HEADS)):
                     cols = slice(HEAD_DIM * h, HEAD_DIM * (h + 1))
-                    factor = rstd[i][:, h : h + 1]
-                    if i == TILES - 1 and h >= VECTOR_HEADS - 2:
-                        nc.vector.tensor_scalar(
-                            out=result[i][:, cols], in0=rotated[:, cols], scalar1=factor, scalar2=None, op0=ALU.mult
-                        )
-                    else:
-                        nc.scalar.activation(
-                            out=result[i][:, cols], in_=rotated[:, cols], func=ACT.Copy, scale=factor
-                        )
-                nc.sync.dma_start(
-                    out=out[n, P * s : P * (s + 1), first:last, :].rearrange("p h c -> p (h c)"),
-                    in_=result[i][:, HEAD_DIM * first : HEAD_DIM * last],
+                    nc.scalar.activation(
+                        out=result[i][:, cols], in_=terms[i][:, 0, cols], func=ACT.Copy, scale=rstd[i][:, h : h + 1]
+                    )
+                store(i, first, last)
+
+        def store(i, first, last):
+            s, n = divmod(i, BATCH)
+            nc.sync.dma_start(
+                out=out[n, P * s : P * (s + 1), first:last, :].rearrange("p h c -> p (h c)"),
+                in_=result[i][:, HEAD_DIM * first : HEAD_DIM * last],
+            )
+
+        def finish_last_tile(i):
+            result[i] = stored.tile([P, CH], F32, name="result")
+            for first, last in LAST_PIECES:
+                if last <= VECTOR_HEADS:
+                    source, base = terms[i], 0
+                else:
+                    source, base = tensor_terms[i], VECTOR_HEADS
+                    products(nc.vector, source, i, base, HEADS - base, tab[i // BATCH])
+                cols = slice(HEAD_DIM * (first - base), HEAD_DIM * (last - base))
+                nc.vector.tensor_tensor(
+                    out=source[:, 0, cols], in0=source[:, 0, cols], in1=source[:, 1, cols], op=ALU.add
                 )
+                for h in range(first, last):
+                    summed = source[:, 0, HEAD_DIM * (h - base) : HEAD_DIM * (h - base + 1)]
+                    scaled = result[i][:, HEAD_DIM * h : HEAD_DIM * (h + 1)]
+                    factor = rstd[i][:, h : h + 1]
+                    if h < VECTOR_HEADS:
+                        nc.scalar.activation(out=scaled, in_=summed, func=ACT.Copy, scale=factor)
+                    else:
+                        nc.vector.tensor_scalar(out=scaled, in0=summed, scalar1=factor, scalar2=None, op0=ALU.mult)
+                store(i, first, last)
 
         def run(stage, i):
             if 0 <= i < TILES:
                 stage(i)
 
-        for step in range(-3, TILES + 1):
+        for step in range(-3, TILES):
             run(add_terms_on_tensor, step - 1)
             run(multiply, step + 1)
             for i in {-2: (), -1: (1, 2)}.get(step, (step + 3,)):
@@ -301,6 +303,9 @@ def tile_selfattention_pa_t_kernel(tc, x, freqs, w_words, w_scales, b, g, out):
             if 1 <= step <= half:
                 build_table(nc.vector, half + step - 1)
             run(statistics, step)
-            run(products_on_gpsimd, step + 1)
-            run(add_terms, step)
+            if step < TILES - 2:
+                run(products_on_gpsimd, step + 1)
+            if step < TILES - 1:
+                run(add_terms, step)
             run(scale_and_store, step - 1)
+        finish_last_tile(TILES - 1)

from contextlib import ExitStack

import concourse.mybir as mybir
from concourse.masks import make_identity

F32 = mybir.dt.float32
BF16 = mybir.dt.bfloat16
I32 = mybir.dt.int32
U32 = mybir.dt.uint32
U8 = mybir.dt.uint8
FP8X4 = mybir.dt.float8_e4m3fn_x4
FP4X4 = mybir.dt.float4_e2m1fn_x4
ACT = mybir.ActivationFunctionType
ALU = mybir.AluOpType

P = 128
BATCH, SEQ, CH = 4, 1024, 1024
HEADS, HEAD_DIM = 8, 128
PAIRS = HEAD_DIM // 2
EPS = 1e-6
K_PASS = 512
PASSES = CH // K_PASS
N_BANK = 512
BANKS = CH // N_BANK
SEQ_TILES = SEQ // P
TILES = SEQ_TILES * BATCH
VECTOR_HEADS = 6
TENSOR_COLS = HEAD_DIM * (HEADS - VECTOR_HEADS)
VECTOR_COLS = HEAD_DIM * VECTOR_HEADS
LAST_PIECES = [(0, VECTOR_HEADS // 2), (VECTOR_HEADS // 2, VECTOR_HEADS), (VECTOR_HEADS, HEADS)]

WARM_UP = 4

FLOPS = 2 * BATCH * SEQ * CH * CH


def tile_selfattention_pa_t_kernel(tc, x, freqs, w_words, w_scales, b, g, out):
    nc = tc.nc
    with ExitStack() as ctx:
        ctx.enter_context(tc.manual_schedule())
        const = ctx.enter_context(tc.tile_pool(name="const", bufs=1))
        x_pool = ctx.enter_context(tc.tile_pool(name="x_pool", bufs=TILES))
        quant = ctx.enter_context(tc.tile_pool(name="quant", bufs=6))
        work = ctx.enter_context(tc.tile_pool(name="work", bufs=6))
        stored = ctx.enter_context(tc.tile_pool(name="stored", bufs=8))
        small = ctx.enter_context(tc.tile_pool(name="small", bufs=8))
        psum_x = ctx.enter_context(tc.psum_pool(name="psum_x", bufs=2))
        psum_acc = ctx.enter_context(tc.psum_pool(name="psum_acc", bufs=2 * BANKS))
        psum_one = ctx.enter_context(tc.psum_pool(name="psum_one", bufs=1))

        def load_x(i):
            x_tile = x_pool.tile([P, CH], BF16, name="x_tile")
            s, n = divmod(i, BATCH)
            nc.sync.dma_start(out=x_tile[:], in_=x[n, P * s : P * (s + 1), :])
            return x_tile

        zeros = const.tile([P, N_BANK], BF16)
        nc.gpsimd.memset(zeros[:].bitcast(I32), 0)
        for i in range(WARM_UP):
            warm = psum_acc.tile([P, N_BANK], F32, name="acc_bank")
            nc.tensor.matmul(out=warm[:], lhsT=zeros[:, :P], rhs=zeros[:], start=True, stop=True)

        x_sb = [load_x(0)]
        row = const.tile([P, CH + HEAD_DIM], BF16)
        nc.vector.memset(row[:].bitcast(I32), 0)
        nc.sync.dma_start(out=row[0:1, :CH], in_=b.unsqueeze(0))
        nc.sync.dma_start(out=row[0:1, CH:], in_=g.unsqueeze(0))
        w_planes = const.tile([P, PASSES, CH], U8, align_bytes=64)
        nc.vector.memset(w_planes[:].rearrange("p g n -> p (g n)").bitcast(I32), 0)
        scale_rows = w_scales.bitcast(I32)
        for quadrant in range(4):
            nc.sync.dma_start(
                out=w_planes[32 * quadrant : 32 * quadrant + 4, :, :].bitcast(I32),
                in_=scale_rows[:, 4 * quadrant : 4 * quadrant + 4, :].rearrange("g r n -> r g n"),
            )
        w_sb = const.tile([P, PASSES, 2 * CH], U8, align_bytes=64)
        nc.sync.dma_start(out=w_sb[:].bitcast(I32), in_=w_words.bitcast(I32).rearrange("g p n -> p g n"))
        freqs_sb = const.tile([P, SEQ_TILES, 4 * PAIRS], BF16)
        freqs_rows = freqs[0, :, 0].rearrange("(s p) j i k -> p s (j i k)", p=P)
        half = SEQ_TILES // 2
        nc.sync.dma_start(out=freqs_sb[:, :1, :], in_=freqs_rows[:, :1, :])
        x_sb.append(load_x(1))
        x_sb.append(load_x(2))
        nc.sync.dma_start(out=freqs_sb[:, 1:half, :], in_=freqs_rows[:, 1:half, :])
        x_sb.append(load_x(3))
        nc.sync.dma_start(out=freqs_sb[:, half:, :], in_=freqs_rows[:, half:, :])
        for i in range(4, TILES):
            x_sb.append(load_x(i))

        ident = const.tile([P, P], F32)
        make_identity(nc, ident[:])
        ones = const.tile([P, P], BF16)
        nc.vector.memset(ones[:], 1.0)
        eps_col = const.tile([P, 1], F32)
        nc.vector.memset(eps_col[:], EPS)

        table = const.tile([P, SEQ_TILES, 2 * HEAD_DIM], F32)

        def build_table(engine, s):
            engine.tensor_tensor(
                out=table[:, s, :].rearrange("p (k j i) -> p k j i", k=2, j=PAIRS, i=2),
                in0=freqs_sb[:, s, :].rearrange("p (j i k) -> p k j i", j=PAIRS, i=2, k=2),
                in1=gain_bc[:]
                .rearrange("p (j k o) -> p k j o", j=PAIRS, k=2, o=1)
                .to_broadcast([P, 2, PAIRS, 2]),
                op=ALU.mult,
            )

        gain_bc = const.tile([P, HEAD_DIM], BF16)
        bias_bc = const.tile([P, CH], BF16)

        def spread_constants():
            for tile, first, width in ((gain_bc, CH, HEAD_DIM), (bias_bc, 0, N_BANK), (bias_bc, N_BANK, N_BANK)):
                spread = psum_acc.tile([P, N_BANK], F32, name="acc_bank")
                nc.tensor.matmul(
                    out=spread[:, :width], lhsT=ones[:], rhs=row[:, first : first + width], start=True, stop=True
                )
                to = first % CH
                nc.scalar.copy(out=tile[:, to : to + width], in_=spread[:, :width])

        tab_bank = psum_one.tile([P, 2, 2 * HEAD_DIM], F32, name="tab_bank")
        sum_bank = psum_one.tile([P, 2, TENSOR_COLS], F32, name="sum_bank")

        xt, grouped, x_codes, x_scales, acc, u_sb, rstd, terms, tensor_terms, tab, result = {}, {}, {}, {}, {}, {}, {}, {}, {}, {}, {}

        def transposes(i):
            x_words = x_sb[i][:].bitcast(F32)
            xt[i] = psum_x.tile([P, PASSES, 2, P], F32, name="xt")
            for gp in range(PASSES):
                for u in range(2):
                    nc.tensor.transpose(
                        xt[i][:, gp, u, :], x_words[:, 256 * gp + u : 256 * (gp + 1) : 2], ident[:]
                    )

        def regroup(i):
            grouped[i] = quant.tile([P, PASSES * P * 4], BF16, align_bytes=64, name="grouped")
            copy = nc.vector.tensor_copy if i == 0 else nc.scalar.copy
            copy(
                out=grouped[i][:].bitcast(F32).rearrange("p (g r u) -> p g r u", g=PASSES, r=P, u=2),
                in_=xt[i][:].rearrange("p g u r -> p g r u"),
            )

        def quantise(i):
            x_codes[i] = quant.tile([P, PASSES * P], U32, align_bytes=64, name="x_codes")
            x_scales[i] = quant.tile([P, PASSES * P], U8, align_bytes=64, name="x_scales")
            nc.vector.quantize_mx(
                out=x_codes[i][:].bitcast(FP8X4), scales=x_scales[i][:], in_=grouped[i][:]
            )

        def multiply(i):
            acc[i] = []
            for bank in range(BANKS):
                acc_bank = psum_acc.tile([P, N_BANK], F32, name="acc_bank")
                for gp in range(PASSES):
                    nc.tensor.matmul_mx(
                        out=acc_bank[:],
                        lhsT=x_codes[i][:, P * gp : P * (gp + 1)].bitcast(FP8X4),
                        lhsT_scale=x_scales[i][:, P * gp : P * (gp + 1)],
                        rhs=w_sb[:, gp, 2 * N_BANK * bank : 2 * N_BANK * (bank + 1)].bitcast(FP4X4),
                        rhs_scale=w_planes[:, gp, N_BANK * bank : N_BANK * (bank + 1)],
                        start=(gp == 0),
                        stop=(gp == PASSES - 1),
                    )
                acc[i].append(acc_bank)

        def table_to_psum(s):
            tab[s] = tab_bank[:, s % 2, :]
            nc.tensor.matmul(out=tab[s], lhsT=ident[:], rhs=table[:, s, :], start=True, stop=True)

        def add_bias(i):
            u_sb[i] = work.tile([P, CH], F32, name="u_sb")
            for bank in range(BANKS):
                cols = slice(N_BANK * bank, N_BANK * (bank + 1))
                nc.vector.tensor_tensor(
                    out=u_sb[i][:, cols], in0=acc[i][bank][:], in1=bias_bc[:, cols], op=ALU.add
                )

        def statistics(i):
            sum_sq = small.tile([P, HEADS], F32, name="sum_sq")
            for h in range(HEADS):
                squares = small.tile([P, HEAD_DIM], BF16, name="squares")
                nc.scalar.activation(
                    out=squares[:],
                    in_=u_sb[i][:, HEAD_DIM * h : HEAD_DIM * (h + 1)],
                    func=ACT.Square,
                    accum_out=sum_sq[:, h : h + 1],
                )
            rstd[i] = small.tile([P, HEADS], F32, name="rstd")
            nc.scalar.activation(
                out=rstd[i][:],
                in_=sum_sq[:],
                func=ACT.Abs_reciprocal_sqrt,
                bias=eps_col[:, 0:1],
                scale=1.0 / HEAD_DIM,
            )

        def products(engine, dest, i, first_head, heads, table_kji):
            cols = slice(HEAD_DIM * first_head, HEAD_DIM * (first_head + heads))
            full = [P, 2, heads, PAIRS, 2]
            engine.tensor_tensor(
                out=dest[:].rearrange("p k (h j i) -> p k h j i", h=heads, j=PAIRS, i=2),
                in0=u_sb[i][:, cols]
                .rearrange("p (h j k o) -> p k h j o", h=heads, j=PAIRS, k=2, o=1)
                .to_broadcast(full),
                in1=table_kji.rearrange("p (k o j i) -> p k o j i", k=2, o=1, j=PAIRS, i=2).to_broadcast(full),
                op=ALU.mult,
            )

        def products_on_vector(i):
            if i == TILES - 1:
                tensor_terms[i] = work.tile([P, 2, TENSOR_COLS], F32, name="tensor_terms")
            terms[i] = work.tile([P, 2, VECTOR_COLS], F32, name="terms")
            products(nc.vector, terms[i], i, 0, VECTOR_HEADS, tab[i // BATCH])

        def products_on_gpsimd(i):
            tensor_terms[i] = work.tile([P, 2, TENSOR_COLS], F32, name="tensor_terms")
            products(nc.gpsimd, tensor_terms[i], i, VECTOR_HEADS, HEADS - VECTOR_HEADS, table[:, i // BATCH, :])

        def add_terms(i):
            nc.gpsimd.tensor_tensor(out=terms[i][:, 0, :], in0=terms[i][:, 0, :], in1=terms[i][:, 1, :], op=ALU.add)

        def add_terms_on_tensor(i):
            for k in range(2):
                nc.tensor.matmul(
                    out=sum_bank[:, i % 2, :],
                    lhsT=ident[:],
                    rhs=tensor_terms[i][:, k, :],
                    start=(k == 0),
                    stop=(k == 1),
                )

        def scale_on_vector(i):
            result[i] = stored.tile([P, CH], F32, name="result")
            heads = HEADS - VECTOR_HEADS
            nc.vector.tensor_tensor(
                out=result[i][:, VECTOR_COLS:].rearrange("p (h c) -> p h c", h=heads),
                in0=sum_bank[:, i % 2, :].rearrange("p (h c) -> p h c", h=heads),
                in1=rstd[i][:, VECTOR_HEADS:].unsqueeze(2).to_broadcast([P, heads, HEAD_DIM]),
                op=ALU.mult,
            )

        def scale_and_store(i):
            pieces = [(0, HEADS)] if i < TILES - 3 else list(reversed(LAST_PIECES))
            for first, last in pieces:
                for h in range(first, min(last, VECTOR_HEADS)):
                    cols = slice(HEAD_DIM * h, HEAD_DIM * (h + 1))
                    nc.scalar.activation(
                        out=result[i][:, cols], in_=terms[i][:, 0, cols], func=ACT.Copy, scale=rstd[i][:, h : h + 1]
                    )
                store(i, first, last)

        def store(i, first, last):
            s, n = divmod(i, BATCH)
            nc.sync.dma_start(
                out=out[n, P * s : P * (s + 1), first:last, :].rearrange("p h c -> p (h c)"),
                in_=result[i][:, HEAD_DIM * first : HEAD_DIM * last],
            )

        def finish_last_tile(i):
            result[i] = stored.tile([P, CH], F32, name="result")
            for first, last in LAST_PIECES:
                if last <= VECTOR_HEADS:
                    source, base = terms[i], 0
                else:
                    source, base = tensor_terms[i], VECTOR_HEADS
                    products(nc.vector, source, i, base, HEADS - base, tab[i // BATCH])
                cols = slice(HEAD_DIM * (first - base), HEAD_DIM * (last - base))
                nc.vector.tensor_tensor(
                    out=source[:, 0, cols], in0=source[:, 0, cols], in1=source[:, 1, cols], op=ALU.add
                )
                for h in range(first, last):
                    summed = source[:, 0, HEAD_DIM * (h - base) : HEAD_DIM * (h - base + 1)]
                    scaled = result[i][:, HEAD_DIM * h : HEAD_DIM * (h + 1)]
                    factor = rstd[i][:, h : h + 1]
                    if h < VECTOR_HEADS:
                        nc.scalar.activation(out=scaled, in_=summed, func=ACT.Copy, scale=factor)
                    else:
                        nc.vector.tensor_scalar(out=scaled, in0=summed, scalar1=factor, scalar2=None, op0=ALU.mult)
                store(i, first, last)

        def run(stage, i):
            if 0 <= i < TILES:
                stage(i)

        for step in range(-3, TILES):
            run(add_terms_on_tensor, step - 1)
            run(multiply, step + 1)
            for i in {-2: (), -1: (1, 2)}.get(step, (step + 3,)):
                run(transposes, i)
            if step == -3:
                spread_constants()
            run(regroup, step + 2)
            run(products_on_vector, step)
            run(scale_on_vector, step - 1)
            if (step + 1) % BATCH == 0 and step + 1 < TILES:
                table_to_psum((step + 1) // BATCH)
            run(add_bias, step + 1)
            run(quantise, step + 2)
            if step == -2:
                build_table(nc.vector, 0)
                for s in range(1, half):
                    build_table(nc.gpsimd, s)
            if 1 <= step <= half:
                build_table(nc.vector, half + step - 1)
            run(statistics, step)
            if step < TILES - 2:
                run(products_on_gpsimd, step + 1)
            if step < TILES - 1:
                run(add_terms, step)
            run(scale_and_store, step - 1)
        finish_last_tile(TILES - 1)
